import numpy as np
import ml_dtypes


def mxq(x, axis, fmt="e4m3"):
    dtype, down = {"e4m3": (ml_dtypes.float8_e4m3fn, 7), "e5m2": (ml_dtypes.float8_e5m2, 14)}[fmt]
    v = np.moveaxis(np.asarray(x, np.float32).astype(ml_dtypes.bfloat16).astype(np.float64), axis, -1)
    blocks = v.reshape(v.shape[:-1] + (-1, 32))
    amax = np.abs(blocks).max(-1, keepdims=True)
    byte = np.maximum(np.where(amax > 0, np.frexp(amax)[1] - 1 + 127, 0) - down, 1)
    scale = np.exp2(byte - 127.0)
    codes = (blocks / scale).astype(np.float32).astype(dtype).astype(np.float64)
    return np.moveaxis((codes * scale).reshape(v.shape), -1, axis)


WIDE = False


def mx_kscale(k):
    if not WIDE:
        return np.ones(k)
    levels = np.array([10, -10, 5, -5, 0])
    a = np.random.permutation(np.resize(levels, k // 512 * 4)).reshape(k // 512, 4)
    idx = np.arange(k)
    return np.exp2(a[idx // 512, idx % 128 // 32])


BF16 = ml_dtypes.bfloat16


def bf(x):
    return np.asarray(x, np.float32).astype(BF16)


def f64(x):
    return np.asarray(x).astype(np.float64)


B, H0, C0, C1, C2, NA, NO = 12, 32, 512, 512, 1024, 4, 64
H1, H2 = H0 // 2, H0 // 4
O = NA * NO


def sigmoid(v):
    return 1.0 / (1.0 + np.exp(-v))


def _draw_level(c, h):
    s = mx_kscale(c)
    f = bf(np.random.standard_normal((B, c, h, h)) * s[None, :, None, None])
    w = bf(np.random.standard_normal((O, c)) / np.sqrt(c) / s[None, :])
    b = bf(np.random.standard_normal(O) * 0.5)
    return f, w, b


def setup_inputs():
    f0, w0, b0 = _draw_level(C0, H0)
    f1, w1, b1 = _draw_level(C1, H1)
    f2, w2, b2 = _draw_level(C2, H2)
    anchors = bf(1.0 + 4.0 * np.random.random((3, NA, 2)))
    return {"f0": f0, "f1": f1, "f2": f2, "w0": w0, "b0": b0, "w1": w1, "b1": b1, "w2": w2, "b2": b2, "anchors": anchors}


def _decode_level(f, w, b, anchors_i):
    nb, c, h, wd = f.shape
    y = (mxq(w, 1, "e4m3") @ mxq(f.reshape(nb, c, h * wd), 1, "e4m3")) + b[None, :, None]
    y = y.reshape(nb, NA, NO, h, wd).transpose(0, 1, 3, 4, 2)
    xy = 2.0 * sigmoid(y[..., 0:2]) - 0.5
    wh = np.square(2.0 * sigmoid(y[..., 2:4])) * anchors_i[None, :, None, None, :]
    rest = y[..., 4:]
    out = np.concatenate([xy, wh, rest], axis=-1)
    return out.reshape(nb, -1, NO)


def reference(f0, f1, f2, w0, b0, w1, b1, w2, b2, anchors):
    a = f64(anchors)
    outs = [
        _decode_level(f64(f0), f64(w0), f64(b0), a[0]),
        _decode_level(f64(f1), f64(w1), f64(b1), a[1]),
        _decode_level(f64(f2), f64(w2), f64(b2), a[2]),
    ]
    return np.concatenate(outs, axis=1)

@@ -1,0 +1,365 @@
+from contextlib import ExitStack
+
+import concourse.bass as bass
+import concourse.mybir as mybir
+import concourse.tile as tile
+from concourse.masks import make_identity
+
+F32 = mybir.dt.float32
+BF16 = mybir.dt.bfloat16
+I32 = mybir.dt.int32
+U32 = mybir.dt.uint32
+U8 = mybir.dt.uint8
+FP8X4 = mybir.dt.float8_e4m3fn_x4
+ACT = mybir.ActivationFunctionType
+ALU = mybir.AluOpType
+
+P = 128
+FLOPS = 2 * 256 * (512 * 12 * 1024 + 512 * 12 * 256 + 1024 * 12 * 64)
+
+MANUAL = False
+STORE_ON_GPSIMD = False
+QS = 100
+RAW_BUFS = 6
+
+
+def tile_head_t_kernel(tc, f0, f1, f2, w0, b0, w1, b1, w2, b2, anchors, out):
+    nc = tc.nc
+    with ExitStack() as ctx:
+        if MANUAL:
+            ctx.enter_context(tc.manual_schedule())
+        const = ctx.enter_context(tc.tile_pool(name="const", bufs=1))
+        rawp = ctx.enter_context(tc.tile_pool(name="rawp", bufs=RAW_BUFS))
+        grpp = ctx.enter_context(tc.tile_pool(name="grpp", bufs=4))
+        codp = ctx.enter_context(tc.tile_pool(name="codp", bufs=3))
+        outp = ctx.enter_context(tc.tile_pool(name="outp", bufs=4))
+        smallp = ctx.enter_context(tc.tile_pool(name="smallp", bufs=3))
+        psum = ctx.enter_context(tc.psum_pool(name="psum", bufs=8))
+        store_eng = nc.gpsimd if STORE_ON_GPSIMD else nc.sync
+
+        ident = const.tile([P, P], F32, name="ident")
+        make_identity(nc, ident[:])
+        ones = const.tile([P, P], BF16, name="ones")
+        nc.vector.memset(ones[:], 1.0)
+        crow = const.tile([P, 800], BF16, name="crow")
+        nc.vector.memset(crow[:].bitcast(I32), 0)
+        for i, b in enumerate((b0, b1, b2)):
+            nc.scalar.dma_start(out=crow[0:1, 256 * i : 256 * (i + 1)], in_=b.unsqueeze(0))
+        nc.scalar.dma_start(out=crow[0:1, 768:792], in_=anchors.rearrange("l a c -> (l a c)").unsqueeze(0))
+        cst = const.tile([P, 800], F32, name="cst")
+        ancx = [const.tile([P, 32, 2], F32, name="ancx%d" % lvl) for lvl in range(3)]
+
+        def spread_constants():
+            cps0 = psum.tile([P, 512], F32, tag="bank", name="cps0")
+            nc.tensor.matmul(out=cps0[:], lhsT=ones[:], rhs=crow[:, 0:512], start=True, stop=True)
+            cps1 = psum.tile([P, 512], F32, tag="bank", name="cps1")
+            nc.tensor.matmul(out=cps1[:, 0:256], lhsT=ones[:], rhs=crow[:, 512:768], start=True, stop=True)
+            nc.tensor.matmul(out=cps1[:, 256:288], lhsT=ones[:], rhs=crow[:, 768:800], start=True, stop=True)
+            nc.vector.tensor_copy(out=cst[:, 0:512], in_=cps0[:])
+            nc.vector.tensor_copy(out=cst[:, 512:800], in_=cps1[:, 0:288])
+            a0 = cst[:, 768:776].rearrange("p (a c) -> p a c", a=4).unsqueeze(2)
+            nc.vector.tensor_copy(
+                out=ancx[0][:].rearrange("p (a t) c -> p a t c", a=4), in_=a0.to_broadcast([P, 4, 8, 2])
+            )
+            a1 = cst[:, 776:784].rearrange("p (a c) -> p a c", a=4).unsqueeze(2)
+            for n in range(4):
+                nc.vector.tensor_copy(
+                    out=ancx[1][:, 8 * n : 8 * n + 8, :].rearrange("p (a t) c -> p a t c", a=4),
+                    in_=a1.to_broadcast([P, 4, 2, 2]),
+                )
+            a2 = cst[:, 784:792].unsqueeze(1)
+            nc.vector.tensor_copy(
+                out=ancx[2][:, 0:12, :].rearrange("p (m a) c -> p m (a c)", m=3), in_=a2.to_broadcast([P, 3, 8])
+            )
+
+        wts = {}
+
+        def load_w(lvl, w, K):
+            w_sb = const.tile([P, 2 * K], BF16, name="w_sb%d" % lvl)
+            nc.sync.dma_start(
+                out=w_sb[:].rearrange("o (b k) -> o b k", b=2), in_=w.rearrange("(b o) k -> o b k", b=2)
+            )
+            wts[lvl] = (w_sb, K)
+
+        def prep_w(lvl):
+            w_sb, K = wts[lvl]
+            passes = K // 512
+            wc = const.tile([P, passes * 256], U32, name="wc%d" % lvl, align_bytes=64)
+            ws = const.tile([P, passes * 256], U8, name="ws%d" % lvl, align_bytes=64)
+            wg = const.tile([P, passes * 1024], BF16, name="wg%d" % lvl, align_bytes=64)
+            words = w_sb[:].bitcast(F32).rearrange("o (b g m u) -> o b g u m", b=2, g=passes, m=128, u=2)
+            for g in range(passes):
+                xt = psum.tile([P, 512], F32, tag="bank", name="xt")
+                for u in range(2):
+                    for b in range(2):
+                        c0 = u * 256 + b * 128
+                        nc.tensor.transpose(xt[:, c0 : c0 + 128], words[:, b, g, u, :], ident[:])
+                nc.vector.tensor_copy(
+                    out=wg[:, g * 1024 : (g + 1) * 1024].bitcast(F32).rearrange("p (o u) -> p o u", u=2),
+                    in_=xt[:].rearrange("p (u o) -> p o u", u=2),
+                )
+            nc.vector.quantize_mx(out=wc[:].bitcast(FP8X4), scales=ws[:], in_=wg[:])
+            wts[lvl] = (wc, ws)
+
+        def mx(ps_cols, cod, scl, c0, lvl, g, start, stop):
+            wc, ws = wts[lvl]
+            nc.tensor.matmul_mx(
+                out=ps_cols,
+                lhsT=cod[:, c0 : c0 + 128].bitcast(FP8X4),
+                lhsT_scale=scl[:, c0 : c0 + 128],
+                rhs=wc[:, g * 256 : (g + 1) * 256].bitcast(FP8X4),
+                rhs_scale=ws[:, g * 256 : (g + 1) * 256],
+                start=start,
+                stop=stop,
+            )
+
+        def small_s(st, rows):
+            rowsv = st["osb"][:, 0 : rows * 64].rearrange("p (r j) -> p r j", j=64)
+            sg = smallp.tile([P, 32, 4], F32, tag="sg", name="sg")
+            sq = smallp.tile([P, 32, 2], F32, tag="sq", name="sq")
+            nc.scalar.activation(out=sg[:, 0:rows, :], in_=rowsv[:, :, 0:4], func=ACT.Sigmoid)
+            nc.scalar.activation(out=sq[:, 0:rows, :], in_=sg[:, 0:rows, 2:4], func=ACT.Square, scale=2.0)
+            st["sg"] = sg
+            st["sq"] = sq
+
+        def small_v(st, rows, lvl):
+            rowsv = st["osb"][:, 0 : rows * 64].rearrange("p (r j) -> p r j", j=64)
+            nc.vector.tensor_scalar(
+                out=rowsv[:, :, 0:2], in0=st["sg"][:, 0:rows, 0:2], scalar1=2.0, scalar2=-0.5, op0=ALU.mult, op1=ALU.add
+            )
+            nc.vector.tensor_tensor(
+                out=rowsv[:, :, 2:4], in0=st["sq"][:, 0:rows, :], in1=ancx[lvl][:, 0:rows, :], op=ALU.mult
+            )
+
+        def bias_at(lvl, t):
+            return (
+                cst[:, 256 * lvl : 256 * (lvl + 1)]
+                .rearrange("p (a j) -> p a j", a=4)
+                .unsqueeze(2)
+                .to_broadcast([P, 4, t, 64])
+            )
+
+        def new_codes(st, width):
+            st["cod"] = codp.tile([P, width], U32, tag="cod", name="cod", align_bytes=64)
+            st["scl"] = codp.tile([P, width], U8, tag="scl", name="scl", align_bytes=64)
+
+        def quant(st, lo, hi):
+            nc.vector.quantize_mx(
+                out=st["cod"][:, lo // 4 : hi // 4].bitcast(FP8X4),
+                scales=st["scl"][:, lo // 4 : hi // 4],
+                in_=st["grp"][:, lo:hi],
+            )
+
+        def make_l0(n):
+            st = {}
+
+            def load():
+                st["raw"] = rawp.tile([P, 4096], BF16, tag="raw", name="raw")
+                nc.sync.dma_start(out=st["raw"][:], in_=f0[n].rearrange("(p j) h w -> p (j h w)", j=4))
+
+            def regroup():
+                st["grp"] = grpp.tile([P, 4096], BF16, tag="grp", name="grp", align_bytes=64)
+                src = st["raw"][:].rearrange("p (j q t) -> p q t j", j=4, q=128, t=8)
+                dst = st["grp"][:].rearrange("p (t q j) -> p q t j", t=8, q=128, j=4)
+                for th in range(2):
+                    nc.scalar.copy(out=dst[:, 0:QS, 4 * th : 4 * th + 4, :], in_=src[:, 0:QS, 4 * th : 4 * th + 4, :])
+                for th in range(2):
+                    nc.vector.tensor_copy(
+                        out=dst[:, QS:128, 4 * th : 4 * th + 4, :], in_=src[:, QS:128, 4 * th : 4 * th + 4, :]
+                    )
+
+            def quant_mm():
+                new_codes(st, 1024)
+                quant(st, 0, 2048)
+                quant(st, 2048, 4096)
+                st["ps"] = []
+                for b in range(4):
+                    ps = psum.tile([P, 512], F32, tag="bank", name="acc")
+                    for i in range(2):
+                        mx(ps[:, 256 * i : 256 * (i + 1)], st["cod"], st["scl"], (2 * b + i) * 128, 0, 0, True, True)
+                    st["ps"].append(ps)
+
+            def evac(part):
+                if part == 0:
+                    st["osb"] = outp.tile([P, 2048], F32, tag="osb", name="osb")
+                ov = st["osb"][:].rearrange("p (a t j) -> p a t j", a=4, t=8, j=64)
+                for b in (2 * part, 2 * part + 1):
+                    nc.vector.tensor_tensor(
+                        out=ov[:, :, 2 * b : 2 * b + 2, :],
+                        in0=st["ps"][b][:].rearrange("p (t a j) -> p a t j", t=2, a=4, j=64),
+                        in1=bias_at(0, 2),
+                        op=ALU.add,
+                    )
+
+            def store():
+                store_eng.dma_start(
+                    out=out[n, 0:4096, :].rearrange("(a q t) j -> q a (t j)", a=4, q=128, t=8),
+                    in_=st["osb"][:].rearrange("p (a x) -> p a x", a=4),
+                )
+
+            return {
+                "load": load, "regroup": regroup, "quant_mm": quant_mm, "evac": evac,
+                "small_s": lambda: small_s(st, 32), "small_v": lambda: small_v(st, 32, 0), "store": store,
+            }
+
+        def make_l1(u, split_load):
+            st = {}
+
+            def load():
+                st["raw"] = rawp.tile([P, 4096], BF16, tag="raw", name="raw")
+                if split_load:
+                    for n in range(4):
+                        nc.sync.dma_start(
+                            out=st["raw"][:, 1024 * n : 1024 * (n + 1)],
+                            in_=f1[4 * u + n].rearrange("(p j) h w -> p (j h w)", j=4),
+                        )
+                else:
+                    nc.sync.dma_start(
+                        out=st["raw"][:].rearrange("p (n x) -> p n x", n=4),
+                        in_=f1[4 * u : 4 * u + 4].rearrange("n (p j) h w -> p n (j h w)", j=4),
+                    )
+
+            def regroup():
+                st["grp"] = grpp.tile([P, 4096], BF16, tag="grp", name="grp", align_bytes=64)
+                for n in range(4):
+                    src = st["raw"][:, 1024 * n : 1024 * (n + 1)].rearrange("p (j q t) -> p q t j", j=4, q=128, t=2)
+                    dst = st["grp"][:, 1024 * n : 1024 * (n + 1)].rearrange("p (t q j) -> p q t j", t=2, q=128, j=4)
+                    if n < 3:
+                        nc.scalar.copy(out=dst, in_=src)
+                    else:
+                        nc.vector.tensor_copy(out=dst, in_=src)
+
+            def quant_mm():
+                new_codes(st, 1024)
+                quant(st, 0, 2048)
+                quant(st, 2048, 4096)
+                st["ps"] = []
+                for n in range(4):
+                    ps = psum.tile([P, 512], F32, tag="bank", name="acc")
+                    for t in range(2):
+                        mx(ps[:, 256 * t : 256 * (t + 1)], st["cod"], st["scl"], (2 * n + t) * 128, 1, 0, True, True)
+                    st["ps"].append(ps)
+
+            def evac(part):
+                if part == 0:
+                    st["osb"] = outp.tile([P, 2048], F32, tag="osb", name="osb")
+                for n in (2 * part, 2 * part + 1):
+                    nc.vector.tensor_tensor(
+                        out=st["osb"][:, 512 * n : 512 * (n + 1)].rearrange("p (a t j) -> p a t j", a=4, t=2, j=64),
+                        in0=st["ps"][n][:].rearrange("p (t a j) -> p a t j", t=2, a=4, j=64),
+                        in1=bias_at(1, 2),
+                        op=ALU.add,
+                    )
+
+            def store():
+                for n in range(4):
+                    store_eng.dma_start(
+                        out=out[4 * u + n, 4096:5120, :].rearrange("(a q t) j -> q a (t j)", a=4, q=128, t=2),
+                        in_=st["osb"][:, 512 * n : 512 * (n + 1)].rearrange("p (a x) -> p a x", a=4),
+                    )
+
+            return {
+                "load": load, "regroup": regroup, "quant_mm": quant_mm, "evac": evac,
+                "small_s": lambda: small_s(st, 32), "small_v": lambda: small_v(st, 32, 1), "store": store,
+            }
+
+        def make_l2(h):
+            st = {}
+
+            def load():
+                st["raw"] = rawp.tile([P, 3072], BF16, tag="raw", name="raw")
+                nc.sync.dma_start(
+                    out=st["raw"][:].rearrange("p (x y) -> p x y", x=12),
+                    in_=f2[6 * h : 6 * h + 6].rearrange("n (g p j) h w -> p (n g) (j h w)", g=2, p=128, j=4),
+                )
+
+            def regroup():
+                st["grp"] = grpp.tile([P, 3072], BF16, tag="grp", name="grp", align_bytes=64)
+                src = st["raw"][:].rearrange("p (n g j s) -> p g n s j", n=6, g=2, j=4, s=64)
+                dst = st["grp"][:].rearrange("p (g n s j) -> p g n s j", g=2, n=6, s=64, j=4)
+                for g in range(2):
+                    nc.scalar.copy(out=dst[:, g, 0:4], in_=src[:, g, 0:4])
+                for g in range(2):
+                    nc.vector.tensor_copy(out=dst[:, g, 4:6], in_=src[:, g, 4:6])
+
+            def quant_mm():
+                new_codes(st, 768)
+                quant(st, 0, 2048)
+                quant(st, 2048, 3072)
+                st["ps"] = []
+                for b in range(2):
+                    ps = psum.tile([P, 512], F32, tag="bank", name="acc")
+                    for i in range(2 - b):
+                        m = 2 * b + i
+                        for g in range(2):
+                            mx(ps[:, 256 * i : 256 * (i + 1)], st["cod"], st["scl"], g * 384 + m * 128, 2, g, g == 0, g == 1)
+                    st["ps"].append(ps)
+
+            def evac(part):
+                if part == 0:
+                    st["osb"] = outp.tile([P, 768], F32, tag="osb", name="osb")
+                    nc.vector.tensor_tensor(
+                        out=st["osb"][:, 0:512].rearrange("p (m x) -> p m x", m=2),
+                        in0=st["ps"][0][:].rearrange("p (m x) -> p m x", m=2),
+                        in1=cst[:, 512:768].unsqueeze(1).to_broadcast([P, 2, 256]),
+                        op=ALU.add,
+                    )
+                else:
+                    nc.vector.tensor_tensor(
+                        out=st["osb"][:, 512:768], in0=st["ps"][1][:, 0:256], in1=cst[:, 512:768], op=ALU.add
+                    )
+
+            def store():
+                for m in range(3):
+                    for n2 in range(2):
+                        store_eng.dma_start(
+                            out=out[6 * h + 2 * m + n2, 5120:5376, :].rearrange("(a s) j -> s a j", a=4),
+                            in_=st["osb"][64 * n2 : 64 * n2 + 64, 256 * m : 256 * (m + 1)].rearrange(
+                                "p (a j) -> p a j", a=4
+                            ),
+                        )
+
+            return {
+                "load": load, "regroup": regroup, "quant_mm": quant_mm, "evac": evac,
+                "small_s": lambda: small_s(st, 12), "small_v": lambda: small_v(st, 12, 2), "store": store,
+            }
+
+        units = [make_l1(u, u == 0) for u in range(3)] + [make_l0(n) for n in range(12)] + [make_l2(h) for h in range(2)]
+        N = len(units)
+
+        load_w(1, w1, 512)
+        units[0]["load"]()
+        load_w(0, w0, 512)
+        units[1]["load"]()
+        units[2]["load"]()
+        units[3]["load"]()
+        load_w(2, w2, 1024)
+        units[4]["load"]()
+        units[5]["load"]()
+        prep_w(1)
+        units[0]["regroup"]()
+        units[6]["load"]()
+        spread_constants()
+        units[1]["regroup"]()
+        units[7]["load"]()
+
+        for k in range(N + 2):
+            if 0 <= k - 2 < N:
+                units[k - 2]["small_s"]()
+            if k < N:
+                units[k]["quant_mm"]()
+            if 0 <= k - 1 < N:
+                units[k - 1]["evac"](0)
+            if k + 2 < N:
+                units[k + 2]["regroup"]()
+            if k + 2 + RAW_BUFS < N:
+                units[k + 2 + RAW_BUFS]["load"]()
+            if 0 <= k - 1 < N:
+                units[k - 1]["evac"](1)
+            if 0 <= k - 2 < N:
+                units[k - 2]["small_v"]()
+                units[k - 2]["store"]()
+            if k == 0:
+                prep_w(0)
+            if k == 1:
+                prep_w(2)

@@ -17,10 +17,12 @@ ALU = mybir.AluOpType
 P = 128
 FLOPS = 2 * 256 * (512 * 12 * 1024 + 512 * 12 * 256 + 1024 * 12 * 64)
 
-MANUAL = False
+MANUAL = True
 STORE_ON_GPSIMD = False
-QS = 100
+QS = 80
 RAW_BUFS = 6
+GRP_BUFS = 2
+Q1 = 80
 
 
 def tile_head_t_kernel(tc, f0, f1, f2, w0, b0, w1, b1, w2, b2, anchors, out):
@@ -30,7 +32,7 @@ def tile_head_t_kernel(tc, f0, f1, f2, w0, b0, w1, b1, w2, b2, anchors, out):
             ctx.enter_context(tc.manual_schedule())
         const = ctx.enter_context(tc.tile_pool(name="const", bufs=1))
         rawp = ctx.enter_context(tc.tile_pool(name="rawp", bufs=RAW_BUFS))
-        grpp = ctx.enter_context(tc.tile_pool(name="grpp", bufs=4))
+        grpp = ctx.enter_context(tc.tile_pool(name="grpp", bufs=GRP_BUFS))
         codp = ctx.enter_context(tc.tile_pool(name="codp", bufs=3))
         outp = ctx.enter_context(tc.tile_pool(name="outp", bufs=4))
         smallp = ctx.enter_context(tc.tile_pool(name="smallp", bufs=3))
@@ -101,6 +103,9 @@ def tile_head_t_kernel(tc, f0, f1, f2, w0, b0, w1, b1, w2, b2, anchors, out):
             nc.vector.quantize_mx(out=wc[:].bitcast(FP8X4), scales=ws[:], in_=wg[:])
             wts[lvl] = (wc, ws)
 
+        def pool_copy(dst, src):
+            nc.gpsimd.tensor_scalar(out=dst, in0=src, scalar1=1.0, scalar2=0.0, op0=ALU.mult, op1=ALU.add)
+
         def mx(ps_cols, cod, scl, c0, lvl, g, start, stop):
             wc, ws = wts[lvl]
             nc.tensor.matmul_mx(
@@ -118,16 +123,14 @@ def tile_head_t_kernel(tc, f0, f1, f2, w0, b0, w1, b1, w2, b2, anchors, out):
             sg = smallp.tile([P, 32, 4], F32, tag="sg", name="sg")
             sq = smallp.tile([P, 32, 2], F32, tag="sq", name="sq")
             nc.scalar.activation(out=sg[:, 0:rows, :], in_=rowsv[:, :, 0:4], func=ACT.Sigmoid)
+            nc.scalar.activation(out=rowsv[:, :, 0:2], in_=sg[:, 0:rows, 0:2], func=ACT.Copy, scale=2.0, bias=-0.5)
             nc.scalar.activation(out=sq[:, 0:rows, :], in_=sg[:, 0:rows, 2:4], func=ACT.Square, scale=2.0)
             st["sg"] = sg
             st["sq"] = sq
 
         def small_v(st, rows, lvl):
             rowsv = st["osb"][:, 0 : rows * 64].rearrange("p (r j) -> p r j", j=64)
-            nc.vector.tensor_scalar(
-                out=rowsv[:, :, 0:2], in0=st["sg"][:, 0:rows, 0:2], scalar1=2.0, scalar2=-0.5, op0=ALU.mult, op1=ALU.add
-            )
-            nc.vector.tensor_tensor(
+            nc.gpsimd.tensor_tensor(
                 out=rowsv[:, :, 2:4], in0=st["sq"][:, 0:rows, :], in1=ancx[lvl][:, 0:rows, :], op=ALU.mult
             )
 
@@ -164,9 +167,7 @@ def tile_head_t_kernel(tc, f0, f1, f2, w0, b0, w1, b1, w2, b2, anchors, out):
                 for th in range(2):
                     nc.scalar.copy(out=dst[:, 0:QS, 4 * th : 4 * th + 4, :], in_=src[:, 0:QS, 4 * th : 4 * th + 4, :])
                 for th in range(2):
-                    nc.vector.tensor_copy(
-                        out=dst[:, QS:128, 4 * th : 4 * th + 4, :], in_=src[:, QS:128, 4 * th : 4 * th + 4, :]
-                    )
+                    pool_copy(dst[:, QS:128, 4 * th : 4 * th + 4, :], src[:, QS:128, 4 * th : 4 * th + 4, :])
 
             def quant_mm():
                 new_codes(st, 1024)
@@ -224,10 +225,8 @@ def tile_head_t_kernel(tc, f0, f1, f2, w0, b0, w1, b1, w2, b2, anchors, out):
                 for n in range(4):
                     src = st["raw"][:, 1024 * n : 1024 * (n + 1)].rearrange("p (j q t) -> p q t j", j=4, q=128, t=2)
                     dst = st["grp"][:, 1024 * n : 1024 * (n + 1)].rearrange("p (t q j) -> p q t j", t=2, q=128, j=4)
-                    if n < 3:
-                        nc.scalar.copy(out=dst, in_=src)
-                    else:
-                        nc.vector.tensor_copy(out=dst, in_=src)
+                    nc.scalar.copy(out=dst[:, 0:Q1], in_=src[:, 0:Q1])
+                    pool_copy(dst[:, Q1:128], src[:, Q1:128])
 
             def quant_mm():
                 new_codes(st, 1024)
@@ -280,7 +279,7 @@ def tile_head_t_kernel(tc, f0, f1, f2, w0, b0, w1, b1, w2, b2, anchors, out):
                 for g in range(2):
                     nc.scalar.copy(out=dst[:, g, 0:4], in_=src[:, g, 0:4])
                 for g in range(2):
-                    nc.vector.tensor_copy(out=dst[:, g, 4:6], in_=src[:, g, 4:6])
+                    pool_copy(dst[:, g, 4:6], src[:, g, 4:6])
 
             def quant_mm():
                 new_codes(st, 768)
@@ -350,12 +349,11 @@ def tile_head_t_kernel(tc, f0, f1, f2, w0, b0, w1, b1, w2, b2, anchors, out):
                 units[k]["quant_mm"]()
             if 0 <= k - 1 < N:
                 units[k - 1]["evac"](0)
+                units[k - 1]["evac"](1)
             if k + 2 < N:
                 units[k + 2]["regroup"]()
             if k + 2 + RAW_BUFS < N:
                 units[k + 2 + RAW_BUFS]["load"]()
-            if 0 <= k - 1 < N:
-                units[k - 1]["evac"](1)
             if 0 <= k - 2 < N:
                 units[k - 2]["small_v"]()
                 units[k - 2]["store"]()

@@ -20,7 +20,8 @@ FLOPS = 2 * 256 * (512 * 12 * 1024 + 512 * 12 * 256 + 1024 * 12 * 64)
 MANUAL = True
 STORE_ON_GPSIMD = False
 QS = 80
-RAW_BUFS = 6
+RAW_BUFS = 8
+OUT_BUFS = 8
 GRP_BUFS = 2
 Q1 = 80
 
@@ -34,7 +35,7 @@ def tile_head_t_kernel(tc, f0, f1, f2, w0, b0, w1, b1, w2, b2, anchors, out):
         rawp = ctx.enter_context(tc.tile_pool(name="rawp", bufs=RAW_BUFS))
         grpp = ctx.enter_context(tc.tile_pool(name="grpp", bufs=GRP_BUFS))
         codp = ctx.enter_context(tc.tile_pool(name="codp", bufs=3))
-        outp = ctx.enter_context(tc.tile_pool(name="outp", bufs=4))
+        outp = ctx.enter_context(tc.tile_pool(name="outp", bufs=OUT_BUFS))
         smallp = ctx.enter_context(tc.tile_pool(name="smallp", bufs=3))
         psum = ctx.enter_context(tc.psum_pool(name="psum", bufs=8))
         store_eng = nc.gpsimd if STORE_ON_GPSIMD else nc.sync
@@ -333,14 +334,14 @@ def tile_head_t_kernel(tc, f0, f1, f2, w0, b0, w1, b1, w2, b2, anchors, out):
         units[2]["load"]()
         units[3]["load"]()
         load_w(2, w2, 1024)
-        units[4]["load"]()
-        units[5]["load"]()
+        for i in range(4, RAW_BUFS):
+            units[i]["load"]()
         prep_w(1)
         units[0]["regroup"]()
-        units[6]["load"]()
+        units[RAW_BUFS]["load"]()
         spread_constants()
         units[1]["regroup"]()
-        units[7]["load"]()
+        units[RAW_BUFS + 1]["load"]()
 
         for k in range(N + 2):
             if 0 <= k - 2 < N:

@@ -19,11 +19,11 @@ FLOPS = 2 * 256 * (512 * 12 * 1024 + 512 * 12 * 256 + 1024 * 12 * 64)
 
 MANUAL = True
 STORE_ON_GPSIMD = False
-QS = 80
+QS = 72
 RAW_BUFS = 8
 OUT_BUFS = 8
 GRP_BUFS = 2
-Q1 = 80
+QG = 104
 
 
 def tile_head_t_kernel(tc, f0, f1, f2, w0, b0, w1, b1, w2, b2, anchors, out):
@@ -168,7 +168,11 @@ def tile_head_t_kernel(tc, f0, f1, f2, w0, b0, w1, b1, w2, b2, anchors, out):
                 for th in range(2):
                     nc.scalar.copy(out=dst[:, 0:QS, 4 * th : 4 * th + 4, :], in_=src[:, 0:QS, 4 * th : 4 * th + 4, :])
                 for th in range(2):
-                    pool_copy(dst[:, QS:128, 4 * th : 4 * th + 4, :], src[:, QS:128, 4 * th : 4 * th + 4, :])
+                    pool_copy(dst[:, QS:QG, 4 * th : 4 * th + 4, :], src[:, QS:QG, 4 * th : 4 * th + 4, :])
+                for th in range(2):
+                    nc.vector.tensor_copy(
+                        out=dst[:, QG:128, 4 * th : 4 * th + 4, :], in_=src[:, QG:128, 4 * th : 4 * th + 4, :]
+                    )
 
             def quant_mm():
                 new_codes(st, 1024)
@@ -226,8 +230,12 @@ def tile_head_t_kernel(tc, f0, f1, f2, w0, b0, w1, b1, w2, b2, anchors, out):
                 for n in range(4):
                     src = st["raw"][:, 1024 * n : 1024 * (n + 1)].rearrange("p (j q t) -> p q t j", j=4, q=128, t=2)
                     dst = st["grp"][:, 1024 * n : 1024 * (n + 1)].rearrange("p (t q j) -> p q t j", t=2, q=128, j=4)
-                    nc.scalar.copy(out=dst[:, 0:Q1], in_=src[:, 0:Q1])
-                    pool_copy(dst[:, Q1:128], src[:, Q1:128])
+                    if n < 2:
+                        nc.scalar.copy(out=dst, in_=src)
+                    elif n == 2:
+                        pool_copy(dst, src)
+                    else:
+                        nc.vector.tensor_copy(out=dst, in_=src)
 
             def quant_mm():
                 new_codes(st, 1024)
@@ -278,9 +286,11 @@ def tile_head_t_kernel(tc, f0, f1, f2, w0, b0, w1, b1, w2, b2, anchors, out):
                 src = st["raw"][:].rearrange("p (n g j s) -> p g n s j", n=6, g=2, j=4, s=64)
                 dst = st["grp"][:].rearrange("p (g n s j) -> p g n s j", g=2, n=6, s=64, j=4)
                 for g in range(2):
-                    nc.scalar.copy(out=dst[:, g, 0:4], in_=src[:, g, 0:4])
+                    nc.scalar.copy(out=dst[:, g, 0:3], in_=src[:, g, 0:3])
                 for g in range(2):
-                    pool_copy(dst[:, g, 4:6], src[:, g, 4:6])
+                    pool_copy(dst[:, g, 3:5], src[:, g, 3:5])
+                for g in range(2):
+                    nc.vector.tensor_copy(out=dst[:, g, 5:6], in_=src[:, g, 5:6])
 
             def quant_mm():
                 new_codes(st, 768)

@@ -23,6 +23,8 @@ QS = 72
 RAW_BUFS = 8
 OUT_BUFS = 8
 GRP_BUFS = 2
+T1S = 5
+T1G = 7
 QG = 104
 
 
@@ -65,11 +67,9 @@ def tile_head_t_kernel(tc, f0, f1, f2, w0, b0, w1, b1, w2, b2, anchors, out):
                 out=ancx[0][:].rearrange("p (a t) c -> p a t c", a=4), in_=a0.to_broadcast([P, 4, 8, 2])
             )
             a1 = cst[:, 776:784].rearrange("p (a c) -> p a c", a=4).unsqueeze(2)
-            for n in range(4):
-                nc.vector.tensor_copy(
-                    out=ancx[1][:, 8 * n : 8 * n + 8, :].rearrange("p (a t) c -> p a t c", a=4),
-                    in_=a1.to_broadcast([P, 4, 2, 2]),
-                )
+            nc.vector.tensor_copy(
+                out=ancx[1][:].rearrange("p (a t) c -> p a t c", a=4), in_=a1.to_broadcast([P, 4, 8, 2])
+            )
             a2 = cst[:, 784:792].unsqueeze(1)
             nc.vector.tensor_copy(
                 out=ancx[2][:, 0:12, :].rearrange("p (m a) c -> p m (a c)", m=3), in_=a2.to_broadcast([P, 3, 8])
@@ -227,34 +227,37 @@ def tile_head_t_kernel(tc, f0, f1, f2, w0, b0, w1, b1, w2, b2, anchors, out):
 
             def regroup():
                 st["grp"] = grpp.tile([P, 4096], BF16, tag="grp", name="grp", align_bytes=64)
+                dst = st["grp"][:].rearrange("p (t q n j) -> p n q t j", t=8, q=32, n=4, j=4)
+                srcs = [
+                    st["raw"][:, 1024 * n : 1024 * (n + 1)].rearrange("p (j q t) -> p q t j", j=4, q=32, t=8)
+                    for n in range(4)
+                ]
                 for n in range(4):
-                    src = st["raw"][:, 1024 * n : 1024 * (n + 1)].rearrange("p (j q t) -> p q t j", j=4, q=128, t=2)
-                    dst = st["grp"][:, 1024 * n : 1024 * (n + 1)].rearrange("p (t q j) -> p q t j", t=2, q=128, j=4)
-                    if n < 2:
-                        nc.scalar.copy(out=dst, in_=src)
-                    elif n == 2:
-                        pool_copy(dst, src)
-                    else:
-                        nc.vector.tensor_copy(out=dst, in_=src)
+                    nc.scalar.copy(out=dst[:, n, :, 0:T1S, :], in_=srcs[n][:, :, 0:T1S, :])
+                for n in range(4):
+                    pool_copy(dst[:, n, :, T1S:T1G, :], srcs[n][:, :, T1S:T1G, :])
+                for n in range(4):
+                    nc.vector.tensor_copy(out=dst[:, n, :, T1G:8, :], in_=srcs[n][:, :, T1G:8, :])
 
             def quant_mm():
                 new_codes(st, 1024)
                 quant(st, 0, 2048)
                 quant(st, 2048, 4096)
                 st["ps"] = []
-                for n in range(4):
+                for b in range(4):
                     ps = psum.tile([P, 512], F32, tag="bank", name="acc")
-                    for t in range(2):
-                        mx(ps[:, 256 * t : 256 * (t + 1)], st["cod"], st["scl"], (2 * n + t) * 128, 1, 0, True, True)
+                    for i in range(2):
+                        mx(ps[:, 256 * i : 256 * (i + 1)], st["cod"], st["scl"], (2 * b + i) * 128, 1, 0, True, True)
                     st["ps"].append(ps)
 
             def evac(part):
                 if part == 0:
                     st["osb"] = outp.tile([P, 2048], F32, tag="osb", name="osb")
-                for n in (2 * part, 2 * part + 1):
+                ov = st["osb"][:].rearrange("p (a t j) -> p a t j", a=4, t=8, j=64)
+                for b in (2 * part, 2 * part + 1):
                     nc.vector.tensor_tensor(
-                        out=st["osb"][:, 512 * n : 512 * (n + 1)].rearrange("p (a t j) -> p a t j", a=4, t=2, j=64),
-                        in0=st["ps"][n][:].rearrange("p (t a j) -> p a t j", t=2, a=4, j=64),
+                        out=ov[:, :, 2 * b : 2 * b + 2, :],
+                        in0=st["ps"][b][:].rearrange("p (t a j) -> p a t j", t=2, a=4, j=64),
                         in1=bias_at(1, 2),
                         op=ALU.add,
                     )
@@ -262,8 +265,8 @@ def tile_head_t_kernel(tc, f0, f1, f2, w0, b0, w1, b1, w2, b2, anchors, out):
             def store():
                 for n in range(4):
                     store_eng.dma_start(
-                        out=out[4 * u + n, 4096:5120, :].rearrange("(a q t) j -> q a (t j)", a=4, q=128, t=2),
-                        in_=st["osb"][:, 512 * n : 512 * (n + 1)].rearrange("p (a x) -> p a x", a=4),
+                        out=out[4 * u + n, 4096:5120, :].rearrange("(a q t) j -> q a (t j)", a=4, q=32, t=8),
+                        in_=st["osb"][n:128:4, :].rearrange("p (a x) -> p a x", a=4),
                     )
 
             return {
@@ -283,14 +286,14 @@ def tile_head_t_kernel(tc, f0, f1, f2, w0, b0, w1, b1, w2, b2, anchors, out):
 
             def regroup():
                 st["grp"] = grpp.tile([P, 3072], BF16, tag="grp", name="grp", align_bytes=64)
-                src = st["raw"][:].rearrange("p (n g j s) -> p g n s j", n=6, g=2, j=4, s=64)
-                dst = st["grp"][:].rearrange("p (g n s j) -> p g n s j", g=2, n=6, s=64, j=4)
-                for g in range(2):
-                    nc.scalar.copy(out=dst[:, g, 0:3], in_=src[:, g, 0:3])
-                for g in range(2):
-                    pool_copy(dst[:, g, 3:5], src[:, g, 3:5])
-                for g in range(2):
-                    nc.vector.tensor_copy(out=dst[:, g, 5:6], in_=src[:, g, 5:6])
+                src = st["raw"][:].rearrange("p (m n g j s) -> p g n m s j", m=3, n=2, g=2, j=4, s=64)
+                dst = st["grp"][:].rearrange("p (g m s n j) -> p g n m s j", g=2, m=3, s=64, n=2, j=4)
+                for n2 in range(2):
+                    nc.scalar.copy(out=dst[:, 0, n2], in_=src[:, 0, n2])
+                for n2 in range(2):
+                    pool_copy(dst[:, 1, n2, 0:2], src[:, 1, n2, 0:2])
+                for n2 in range(2):
+                    nc.vector.tensor_copy(out=dst[:, 1, n2, 2:3], in_=src[:, 1, n2, 2:3])
 
             def quant_mm():
                 new_codes(st, 768)
@@ -324,7 +327,7 @@ def tile_head_t_kernel(tc, f0, f1, f2, w0, b0, w1, b1, w2, b2, anchors, out):
                     for n2 in range(2):
                         store_eng.dma_start(
                             out=out[6 * h + 2 * m + n2, 5120:5376, :].rearrange("(a s) j -> s a j", a=4),
-                            in_=st["osb"][64 * n2 : 64 * n2 + 64, 256 * m : 256 * (m + 1)].rearrange(
+                            in_=st["osb"][n2:128:2, 256 * m : 256 * (m + 1)].rearrange(
                                 "p (a j) -> p a j", a=4
                             ),
                         )

@@ -1,8 +1,6 @@
 from contextlib import ExitStack
 
-import concourse.bass as bass
 import concourse.mybir as mybir
-import concourse.tile as tile
 from concourse.masks import make_identity
 
 F32 = mybir.dt.float32
@@ -17,30 +15,28 @@ ALU = mybir.AluOpType
 P = 128
 FLOPS = 2 * 256 * (512 * 12 * 1024 + 512 * 12 * 256 + 1024 * 12 * 64)
 
-MANUAL = True
-STORE_ON_GPSIMD = False
-QS = 72
+FORM_A = True
+L1_NEW = True
+ORDER = "L0first"
+SPLIT = (76, 112)
+HEAD_SPLITS = ((48, 72), (64, 96))
+Q1S = 24
 RAW_BUFS = 8
 OUT_BUFS = 8
-GRP_BUFS = 2
-T1S = 5
-T1G = 7
-QG = 104
+W_STEPS = (6, 9)
 
 
 def tile_head_t_kernel(tc, f0, f1, f2, w0, b0, w1, b1, w2, b2, anchors, out):
     nc = tc.nc
     with ExitStack() as ctx:
-        if MANUAL:
-            ctx.enter_context(tc.manual_schedule())
+        ctx.enter_context(tc.manual_schedule())
         const = ctx.enter_context(tc.tile_pool(name="const", bufs=1))
         rawp = ctx.enter_context(tc.tile_pool(name="rawp", bufs=RAW_BUFS))
-        grpp = ctx.enter_context(tc.tile_pool(name="grpp", bufs=GRP_BUFS))
+        grpp = ctx.enter_context(tc.tile_pool(name="grpp", bufs=2))
         codp = ctx.enter_context(tc.tile_pool(name="codp", bufs=3))
         outp = ctx.enter_context(tc.tile_pool(name="outp", bufs=OUT_BUFS))
         smallp = ctx.enter_context(tc.tile_pool(name="smallp", bufs=3))
         psum = ctx.enter_context(tc.psum_pool(name="psum", bufs=8))
-        store_eng = nc.gpsimd if STORE_ON_GPSIMD else nc.sync
 
         ident = const.tile([P, P], F32, name="ident")
         make_identity(nc, ident[:])
@@ -63,15 +59,22 @@ def tile_head_t_kernel(tc, f0, f1, f2, w0, b0, w1, b1, w2, b2, anchors, out):
             nc.vector.tensor_copy(out=cst[:, 0:512], in_=cps0[:])
             nc.vector.tensor_copy(out=cst[:, 512:800], in_=cps1[:, 0:288])
             a0 = cst[:, 768:776].rearrange("p (a c) -> p a c", a=4).unsqueeze(2)
-            nc.vector.tensor_copy(
+            nc.gpsimd.tensor_copy(
                 out=ancx[0][:].rearrange("p (a t) c -> p a t c", a=4), in_=a0.to_broadcast([P, 4, 8, 2])
             )
             a1 = cst[:, 776:784].rearrange("p (a c) -> p a c", a=4).unsqueeze(2)
-            nc.vector.tensor_copy(
-                out=ancx[1][:].rearrange("p (a t) c -> p a t c", a=4), in_=a1.to_broadcast([P, 4, 8, 2])
-            )
+            if L1_NEW:
+                nc.gpsimd.tensor_copy(
+                    out=ancx[1][:].rearrange("p (a t) c -> p a t c", a=4), in_=a1.to_broadcast([P, 4, 8, 2])
+                )
+            else:
+                for n in range(4):
+                    nc.gpsimd.tensor_copy(
+                        out=ancx[1][:, 8 * n : 8 * n + 8, :].rearrange("p (a t) c -> p a t c", a=4),
+                        in_=a1.to_broadcast([P, 4, 2, 2]),
+                    )
             a2 = cst[:, 784:792].unsqueeze(1)
-            nc.vector.tensor_copy(
+            nc.gpsimd.tensor_copy(
                 out=ancx[2][:, 0:12, :].rearrange("p (m a) c -> p m (a c)", m=3), in_=a2.to_broadcast([P, 3, 8])
             )
 
@@ -84,7 +87,7 @@ def tile_head_t_kernel(tc, f0, f1, f2, w0, b0, w1, b1, w2, b2, anchors, out):
             )
             wts[lvl] = (w_sb, K)
 
-        def prep_w(lvl):
+        def prep_w_a(lvl, on_scalar):
             w_sb, K = wts[lvl]
             passes = K // 512
             wc = const.tile([P, passes * 256], U32, name="wc%d" % lvl, align_bytes=64)
@@ -97,22 +100,27 @@ def tile_head_t_kernel(tc, f0, f1, f2, w0, b0, w1, b1, w2, b2, anchors, out):
                     for b in range(2):
                         c0 = u * 256 + b * 128
                         nc.tensor.transpose(xt[:, c0 : c0 + 128], words[:, b, g, u, :], ident[:])
-                nc.vector.tensor_copy(
-                    out=wg[:, g * 1024 : (g + 1) * 1024].bitcast(F32).rearrange("p (o u) -> p o u", u=2),
-                    in_=xt[:].rearrange("p (u o) -> p o u", u=2),
-                )
+                wgv = wg[:, g * 1024 : (g + 1) * 1024].bitcast(F32).rearrange("p (o u) -> p o u", u=2)
+                if on_scalar:
+                    nc.scalar.copy(out=wgv, in_=xt[:].rearrange("p (u o) -> p o u", u=2))
+                else:
+                    nc.vector.tensor_copy(out=wgv, in_=xt[:].rearrange("p (u o) -> p o u", u=2))
+            wts[lvl] = (wc, ws, wg)
+
+        def prep_w_b(lvl):
+            wc, ws, wg = wts[lvl]
             nc.vector.quantize_mx(out=wc[:].bitcast(FP8X4), scales=ws[:], in_=wg[:])
             wts[lvl] = (wc, ws)
 
         def pool_copy(dst, src):
             nc.gpsimd.tensor_scalar(out=dst, in0=src, scalar1=1.0, scalar2=0.0, op0=ALU.mult, op1=ALU.add)
 
-        def mx(ps_cols, cod, scl, c0, lvl, g, start, stop):
+        def mx(ps_cols, st, c0, lvl, g, start, stop):
             wc, ws = wts[lvl]
             nc.tensor.matmul_mx(
                 out=ps_cols,
-                lhsT=cod[:, c0 : c0 + 128].bitcast(FP8X4),
-                lhsT_scale=scl[:, c0 : c0 + 128],
+                lhsT=st["cod"][:, c0 : c0 + 128].bitcast(FP8X4),
+                lhsT_scale=st["scl"][:, c0 : c0 + 128],
                 rhs=wc[:, g * 256 : (g + 1) * 256].bitcast(FP8X4),
                 rhs_scale=ws[:, g * 256 : (g + 1) * 256],
                 start=start,
@@ -126,36 +134,55 @@ def tile_head_t_kernel(tc, f0, f1, f2, w0, b0, w1, b1, w2, b2, anchors, out):
             nc.scalar.activation(out=sg[:, 0:rows, :], in_=rowsv[:, :, 0:4], func=ACT.Sigmoid)
             nc.scalar.activation(out=rowsv[:, :, 0:2], in_=sg[:, 0:rows, 0:2], func=ACT.Copy, scale=2.0, bias=-0.5)
             nc.scalar.activation(out=sq[:, 0:rows, :], in_=sg[:, 0:rows, 2:4], func=ACT.Square, scale=2.0)
-            st["sg"] = sg
             st["sq"] = sq
 
-        def small_v(st, rows, lvl):
+        def small_g(st, rows, lvl):
             rowsv = st["osb"][:, 0 : rows * 64].rearrange("p (r j) -> p r j", j=64)
             nc.gpsimd.tensor_tensor(
                 out=rowsv[:, :, 2:4], in0=st["sq"][:, 0:rows, :], in1=ancx[lvl][:, 0:rows, :], op=ALU.mult
             )
 
-        def bias_at(lvl, t):
+        def bias_at(lvl):
             return (
                 cst[:, 256 * lvl : 256 * (lvl + 1)]
                 .rearrange("p (a j) -> p a j", a=4)
                 .unsqueeze(2)
-                .to_broadcast([P, 4, t, 64])
+                .to_broadcast([P, 4, 2, 64])
             )
 
-        def new_codes(st, width):
-            st["cod"] = codp.tile([P, width], U32, tag="cod", name="cod", align_bytes=64)
-            st["scl"] = codp.tile([P, width], U8, tag="scl", name="scl", align_bytes=64)
+        def quant(st, width, cuts):
+            st["cod"] = codp.tile([P, width // 4], U32, tag="cod", name="cod", align_bytes=64)
+            st["scl"] = codp.tile([P, width // 4], U8, tag="scl", name="scl", align_bytes=64)
+            for lo, hi in cuts:
+                nc.vector.quantize_mx(
+                    out=st["cod"][:, lo // 4 : hi // 4].bitcast(FP8X4),
+                    scales=st["scl"][:, lo // 4 : hi // 4],
+                    in_=st["grp"][:, lo:hi],
+                )
 
-        def quant(st, lo, hi):
-            nc.vector.quantize_mx(
-                out=st["cod"][:, lo // 4 : hi // 4].bitcast(FP8X4),
-                scales=st["scl"][:, lo // 4 : hi // 4],
-                in_=st["grp"][:, lo:hi],
-            )
+        def eight_tiles(st, lvl):
+            quant(st, 4096, ((0, 2048), (2048, 4096)))
+            st["ps"] = []
+            for b in range(4):
+                ps = psum.tile([P, 512], F32, tag="bank", name="acc")
+                for i in range(2):
+                    mx(ps[:, 256 * i : 256 * (i + 1)], st, (2 * b + i) * 128, lvl, 0, True, True)
+                st["ps"].append(ps)
 
-        def make_l0(n):
+        def evac_rows8(st, lvl):
+            st["osb"] = outp.tile([P, 2048], F32, tag="osb", name="osb")
+            ov = st["osb"][:].rearrange("p (a t j) -> p a t j", a=4, t=8, j=64)
+            for b in range(4):
+                nc.vector.tensor_tensor(
+                    out=ov[:, :, 2 * b : 2 * b + 2, :],
+                    in0=st["ps"][b][:].rearrange("p (t a j) -> p a t j", t=2, a=4, j=64),
+                    in1=bias_at(lvl),
+                    op=ALU.add,
+                )
+
+        def make_l0(n, split):
             st = {}
+            qs, qg = split
 
             def load():
                 st["raw"] = rawp.tile([P, 4096], BF16, tag="raw", name="raw")
@@ -163,49 +190,36 @@ def tile_head_t_kernel(tc, f0, f1, f2, w0, b0, w1, b1, w2, b2, anchors, out):
 
             def regroup():
                 st["grp"] = grpp.tile([P, 4096], BF16, tag="grp", name="grp", align_bytes=64)
-                src = st["raw"][:].rearrange("p (j q t) -> p q t j", j=4, q=128, t=8)
-                dst = st["grp"][:].rearrange("p (t q j) -> p q t j", t=8, q=128, j=4)
+                src_c = st["raw"][:].rearrange("p (j q t) -> p q t j", j=4, q=128, t=8)
+                dst_c = st["grp"][:].rearrange("p (t q j) -> p q t j", t=8, q=128, j=4)
+                src_a = st["raw"][:].rearrange("p (j q t) -> p q j t", j=4, q=128, t=8)
+                dst_a = st["grp"][:].rearrange("p (t q j) -> p q j t", t=8, q=128, j=4)
                 for th in range(2):
-                    nc.scalar.copy(out=dst[:, 0:QS, 4 * th : 4 * th + 4, :], in_=src[:, 0:QS, 4 * th : 4 * th + 4, :])
+                    ts = slice(4 * th, 4 * th + 4)
+                    if FORM_A:
+                        nc.scalar.copy(out=dst_a[:, 0:qs, :, ts], in_=src_a[:, 0:qs, :, ts])
+                    else:
+                        nc.scalar.copy(out=dst_c[:, 0:qs, ts, :], in_=src_c[:, 0:qs, ts, :])
                 for th in range(2):
-                    pool_copy(dst[:, QS:QG, 4 * th : 4 * th + 4, :], src[:, QS:QG, 4 * th : 4 * th + 4, :])
+                    ts = slice(4 * th, 4 * th + 4)
+                    pool_copy(dst_c[:, qs:qg, ts, :], src_c[:, qs:qg, ts, :])
                 for th in range(2):
-                    nc.vector.tensor_copy(
-                        out=dst[:, QG:128, 4 * th : 4 * th + 4, :], in_=src[:, QG:128, 4 * th : 4 * th + 4, :]
-                    )
-
-            def quant_mm():
-                new_codes(st, 1024)
-                quant(st, 0, 2048)
-                quant(st, 2048, 4096)
-                st["ps"] = []
-                for b in range(4):
-                    ps = psum.tile([P, 512], F32, tag="bank", name="acc")
-                    for i in range(2):
-                        mx(ps[:, 256 * i : 256 * (i + 1)], st["cod"], st["scl"], (2 * b + i) * 128, 0, 0, True, True)
-                    st["ps"].append(ps)
-
-            def evac(part):
-                if part == 0:
-                    st["osb"] = outp.tile([P, 2048], F32, tag="osb", name="osb")
-                ov = st["osb"][:].rearrange("p (a t j) -> p a t j", a=4, t=8, j=64)
-                for b in (2 * part, 2 * part + 1):
-                    nc.vector.tensor_tensor(
-                        out=ov[:, :, 2 * b : 2 * b + 2, :],
-                        in0=st["ps"][b][:].rearrange("p (t a j) -> p a t j", t=2, a=4, j=64),
-                        in1=bias_at(0, 2),
-                        op=ALU.add,
-                    )
+                    ts = slice(4 * th, 4 * th + 4)
+                    if FORM_A:
+                        nc.vector.tensor_copy(out=dst_a[:, qg:128, :, ts], in_=src_a[:, qg:128, :, ts])
+                    else:
+                        nc.vector.tensor_copy(out=dst_c[:, qg:128, ts, :], in_=src_c[:, qg:128, ts, :])
 
             def store():
-                store_eng.dma_start(
+                nc.sync.dma_start(
                     out=out[n, 0:4096, :].rearrange("(a q t) j -> q a (t j)", a=4, q=128, t=8),
                     in_=st["osb"][:].rearrange("p (a x) -> p a x", a=4),
                 )
 
             return {
-                "load": load, "regroup": regroup, "quant_mm": quant_mm, "evac": evac,
-                "small_s": lambda: small_s(st, 32), "small_v": lambda: small_v(st, 32, 0), "store": store,
+                "load": load, "regroup": regroup, "quant_mm": lambda: eight_tiles(st, 0),
+                "evac": lambda: evac_rows8(st, 0), "small_s": lambda: small_s(st, 32),
+                "small_g": lambda: small_g(st, 32, 0), "store": store,
             }
 
         def make_l1(u, split_load):
@@ -225,53 +239,58 @@ def tile_head_t_kernel(tc, f0, f1, f2, w0, b0, w1, b1, w2, b2, anchors, out):
                         in_=f1[4 * u : 4 * u + 4].rearrange("n (p j) h w -> p n (j h w)", j=4),
                     )
 
-            def regroup():
+            def regroup_new():
                 st["grp"] = grpp.tile([P, 4096], BF16, tag="grp", name="grp", align_bytes=64)
-                dst = st["grp"][:].rearrange("p (t q n j) -> p n q t j", t=8, q=32, n=4, j=4)
-                srcs = [
-                    st["raw"][:, 1024 * n : 1024 * (n + 1)].rearrange("p (j q t) -> p q t j", j=4, q=32, t=8)
-                    for n in range(4)
-                ]
-                for n in range(4):
-                    nc.scalar.copy(out=dst[:, n, :, 0:T1S, :], in_=srcs[n][:, :, 0:T1S, :])
-                for n in range(4):
-                    pool_copy(dst[:, n, :, T1S:T1G, :], srcs[n][:, :, T1S:T1G, :])
-                for n in range(4):
-                    nc.vector.tensor_copy(out=dst[:, n, :, T1G:8, :], in_=srcs[n][:, :, T1G:8, :])
+                src = st["raw"][:].rearrange("p (i q t) -> p q i t", i=16, q=32, t=8)
+                dst = st["grp"][:].rearrange("p (t q i) -> p q i t", t=8, q=32, i=16)
+                for th in range(2):
+                    ts = slice(4 * th, 4 * th + 4)
+                    nc.scalar.copy(out=dst[:, 0:Q1S, :, ts], in_=src[:, 0:Q1S, :, ts])
+                for th in range(2):
+                    ts = slice(4 * th, 4 * th + 4)
+                    nc.vector.tensor_copy(out=dst[:, Q1S:32, :, ts], in_=src[:, Q1S:32, :, ts])
 
-            def quant_mm():
-                new_codes(st, 1024)
-                quant(st, 0, 2048)
-                quant(st, 2048, 4096)
-                st["ps"] = []
-                for b in range(4):
-                    ps = psum.tile([P, 512], F32, tag="bank", name="acc")
-                    for i in range(2):
-                        mx(ps[:, 256 * i : 256 * (i + 1)], st["cod"], st["scl"], (2 * b + i) * 128, 1, 0, True, True)
-                    st["ps"].append(ps)
+            def regroup_old():
+                st["grp"] = grpp.tile([P, 4096], BF16, tag="grp", name="grp", align_bytes=64)
+                for n in range(4):
+                    src = st["raw"][:, 1024 * n : 1024 * (n + 1)].rearrange("p (j q t) -> p q t j", j=4, q=128, t=2)
+                    dst = st["grp"][:, 1024 * n : 1024 * (n + 1)].rearrange("p (t q j) -> p q t j", t=2, q=128, j=4)
+                    if n < 2:
+                        nc.scalar.copy(out=dst, in_=src)
+                    elif n == 2:
+                        pool_copy(dst, src)
+                    else:
+                        nc.scalar.copy(out=dst[:, 0:64], in_=src[:, 0:64])
+                        nc.vector.tensor_copy(out=dst[:, 64:128], in_=src[:, 64:128])
 
-            def evac(part):
-                if part == 0:
-                    st["osb"] = outp.tile([P, 2048], F32, tag="osb", name="osb")
-                ov = st["osb"][:].rearrange("p (a t j) -> p a t j", a=4, t=8, j=64)
-                for b in (2 * part, 2 * part + 1):
+            def evac_old():
+                st["osb"] = outp.tile([P, 2048], F32, tag="osb", name="osb")
+                for n in range(4):
                     nc.vector.tensor_tensor(
-                        out=ov[:, :, 2 * b : 2 * b + 2, :],
-                        in0=st["ps"][b][:].rearrange("p (t a j) -> p a t j", t=2, a=4, j=64),
-                        in1=bias_at(1, 2),
+                        out=st["osb"][:, 512 * n : 512 * (n + 1)].rearrange("p (a t j) -> p a t j", a=4, t=2, j=64),
+                        in0=st["ps"][n][:].rearrange("p (t a j) -> p a t j", t=2, a=4, j=64),
+                        in1=bias_at(1),
                         op=ALU.add,
                     )
 
             def store():
                 for n in range(4):
-                    store_eng.dma_start(
-                        out=out[4 * u + n, 4096:5120, :].rearrange("(a q t) j -> q a (t j)", a=4, q=32, t=8),
-                        in_=st["osb"][n:128:4, :].rearrange("p (a x) -> p a x", a=4),
-                    )
+                    if L1_NEW:
+                        nc.sync.dma_start(
+                            out=out[4 * u + n, 4096:5120, :].rearrange("(a q t) j -> q a (t j)", a=4, q=32, t=8),
+                            in_=st["osb"][n:128:4, :].rearrange("p (a x) -> p a x", a=4),
+                        )
+                    else:
+                        nc.sync.dma_start(
+                            out=out[4 * u + n, 4096:5120, :].rearrange("(a q t) j -> q a (t j)", a=4, q=128, t=2),
+                            in_=st["osb"][:, 512 * n : 512 * (n + 1)].rearrange("p (a x) -> p a x", a=4),
+                        )
 
             return {
-                "load": load, "regroup": regroup, "quant_mm": quant_mm, "evac": evac,
-                "small_s": lambda: small_s(st, 32), "small_v": lambda: small_v(st, 32, 1), "store": store,
+                "load": load, "regroup": regroup_new if L1_NEW else regroup_old,
+                "quant_mm": lambda: eight_tiles(st, 1),
+                "evac": (lambda: evac_rows8(st, 1)) if L1_NEW else evac_old,
+                "small_s": lambda: small_s(st, 32), "small_g": lambda: small_g(st, 32, 1), "store": store,
             }
 
         def make_l2(h):
@@ -286,92 +305,101 @@ def tile_head_t_kernel(tc, f0, f1, f2, w0, b0, w1, b1, w2, b2, anchors, out):
 
             def regroup():
                 st["grp"] = grpp.tile([P, 3072], BF16, tag="grp", name="grp", align_bytes=64)
-                src = st["raw"][:].rearrange("p (m n g j s) -> p g n m s j", m=3, n=2, g=2, j=4, s=64)
-                dst = st["grp"][:].rearrange("p (g m s n j) -> p g n m s j", g=2, m=3, s=64, n=2, j=4)
-                for n2 in range(2):
-                    nc.scalar.copy(out=dst[:, 0, n2], in_=src[:, 0, n2])
-                for n2 in range(2):
-                    pool_copy(dst[:, 1, n2, 0:2], src[:, 1, n2, 0:2])
-                for n2 in range(2):
-                    nc.vector.tensor_copy(out=dst[:, 1, n2, 2:3], in_=src[:, 1, n2, 2:3])
+                src = st["raw"][:].rearrange("p (n g j s) -> p g n s j", n=6, g=2, j=4, s=64)
+                dst = st["grp"][:].rearrange("p (g n s j) -> p g n s j", g=2, n=6, s=64, j=4)
+                for g in range(2):
+                    nc.scalar.copy(out=dst[:, g, 0:3], in_=src[:, g, 0:3])
+                for g in range(2):
+                    pool_copy(dst[:, g, 3:5], src[:, g, 3:5])
+                for g in range(2):
+                    nc.vector.tensor_copy(out=dst[:, g, 5:6], in_=src[:, g, 5:6])
 
             def quant_mm():
-                new_codes(st, 768)
-                quant(st, 0, 2048)
-                quant(st, 2048, 3072)
+                quant(st, 3072, ((0, 2048), (2048, 3072)))
                 st["ps"] = []
                 for b in range(2):
                     ps = psum.tile([P, 512], F32, tag="bank", name="acc")
                     for i in range(2 - b):
                         m = 2 * b + i
                         for g in range(2):
-                            mx(ps[:, 256 * i : 256 * (i + 1)], st["cod"], st["scl"], g * 384 + m * 128, 2, g, g == 0, g == 1)
+                            mx(ps[:, 256 * i : 256 * (i + 1)], st, g * 384 + m * 128, 2, g, g == 0, g == 1)
                     st["ps"].append(ps)
 
-            def evac(part):
-                if part == 0:
-                    st["osb"] = outp.tile([P, 768], F32, tag="osb", name="osb")
-                    nc.vector.tensor_tensor(
-                        out=st["osb"][:, 0:512].rearrange("p (m x) -> p m x", m=2),
-                        in0=st["ps"][0][:].rearrange("p (m x) -> p m x", m=2),
-                        in1=cst[:, 512:768].unsqueeze(1).to_broadcast([P, 2, 256]),
-                        op=ALU.add,
-                    )
-                else:
-                    nc.vector.tensor_tensor(
-                        out=st["osb"][:, 512:768], in0=st["ps"][1][:, 0:256], in1=cst[:, 512:768], op=ALU.add
-                    )
+            def evac():
+                st["osb"] = outp.tile([P, 768], F32, tag="osb", name="osb")
+                nc.vector.tensor_tensor(
+                    out=st["osb"][:, 0:512].rearrange("p (m x) -> p m x", m=2),
+                    in0=st["ps"][0][:].rearrange("p (m x) -> p m x", m=2),
+                    in1=cst[:, 512:768].unsqueeze(1).to_broadcast([P, 2, 256]),
+                    op=ALU.add,
+                )
+                nc.vector.tensor_tensor(
+                    out=st["osb"][:, 512:768], in0=st["ps"][1][:, 0:256], in1=cst[:, 512:768], op=ALU.add
+                )
 
             def store():
                 for m in range(3):
                     for n2 in range(2):
-                        store_eng.dma_start(
+                        nc.sync.dma_start(
                             out=out[6 * h + 2 * m + n2, 5120:5376, :].rearrange("(a s) j -> s a j", a=4),
-                            in_=st["osb"][n2:128:2, 256 * m : 256 * (m + 1)].rearrange(
+                            in_=st["osb"][64 * n2 : 64 * n2 + 64, 256 * m : 256 * (m + 1)].rearrange(
                                 "p (a j) -> p a j", a=4
                             ),
                         )
 
             return {
                 "load": load, "regroup": regroup, "quant_mm": quant_mm, "evac": evac,
-                "small_s": lambda: small_s(st, 12), "small_v": lambda: small_v(st, 12, 2), "store": store,
+                "small_s": lambda: small_s(st, 12), "small_g": lambda: small_g(st, 12, 2), "store": store,
             }
 
-        units = [make_l1(u, u == 0) for u in range(3)] + [make_l0(n) for n in range(12)] + [make_l2(h) for h in range(2)]
+        wsrc = {0: (w0, 512), 1: (w1, 512), 2: (w2, 1024)}
+        if ORDER == "L1first":
+            units = [make_l1(u, u < 2) for u in range(3)] + [make_l0(n, SPLIT) for n in range(12)]
+            lv = (1, 0, 2)
+        else:
+            units = [make_l0(n, HEAD_SPLITS[n] if n < len(HEAD_SPLITS) else SPLIT) for n in range(12)]
+            units = units + [make_l1(u, False) for u in range(3)]
+            lv = (0, 1, 2)
+        units = units + [make_l2(h) for h in range(2)]
         N = len(units)
 
-        load_w(1, w1, 512)
+        load_w(lv[0], wsrc[lv[0]][0], wsrc[lv[0]][1])
         units[0]["load"]()
-        load_w(0, w0, 512)
         units[1]["load"]()
+        load_w(lv[1], wsrc[lv[1]][0], wsrc[lv[1]][1])
         units[2]["load"]()
         units[3]["load"]()
-        load_w(2, w2, 1024)
+        load_w(lv[2], wsrc[lv[2]][0], wsrc[lv[2]][1])
         for i in range(4, RAW_BUFS):
             units[i]["load"]()
-        prep_w(1)
+        prep_w_a(lv[0], False)
+        prep_w_b(lv[0])
         units[0]["regroup"]()
         units[RAW_BUFS]["load"]()
         spread_constants()
+        units[0]["quant_mm"]()
         units[1]["regroup"]()
         units[RAW_BUFS + 1]["load"]()
 
         for k in range(N + 2):
             if 0 <= k - 2 < N:
                 units[k - 2]["small_s"]()
-            if k < N:
+            if 0 < k < N:
                 units[k]["quant_mm"]()
             if 0 <= k - 1 < N:
-                units[k - 1]["evac"](0)
-                units[k - 1]["evac"](1)
+                units[k - 1]["evac"]()
             if k + 2 < N:
                 units[k + 2]["regroup"]()
             if k + 2 + RAW_BUFS < N:
                 units[k + 2 + RAW_BUFS]["load"]()
             if 0 <= k - 2 < N:
-                units[k - 2]["small_v"]()
+                units[k - 2]["small_g"]()
                 units[k - 2]["store"]()
-            if k == 0:
-                prep_w(0)
-            if k == 1:
-                prep_w(2)
+            if k == W_STEPS[0]:
+                prep_w_a(lv[1], W_STEPS[0] > 2)
+            if k == W_STEPS[0] + 1:
+                prep_w_b(lv[1])
+            if k == W_STEPS[1]:
+                prep_w_a(lv[2], True)
+            if k == W_STEPS[1] + 1:
+                prep_w_b(lv[2])

@@ -248,7 +248,7 @@ def tile_head_t_kernel(tc, f0, f1, f2, w0, b0, w1, b1, w2, b2, anchors, out):
                     nc.scalar.copy(out=dst[:, 0:Q1S, :, ts], in_=src[:, 0:Q1S, :, ts])
                 for th in range(2):
                     ts = slice(4 * th, 4 * th + 4)
-                    nc.vector.tensor_copy(out=dst[:, Q1S:32, :, ts], in_=src[:, Q1S:32, :, ts])
+                    pool_copy(dst[:, Q1S:32, :, ts], src[:, Q1S:32, :, ts])
 
             def regroup_old():
                 st["grp"] = grpp.tile([P, 4096], BF16, tag="grp", name="grp", align_bytes=64)

@@ -18,7 +18,8 @@ FLOPS = 2 * 256 * (512 * 12 * 1024 + 512 * 12 * 256 + 1024 * 12 * 64)
 FORM_A = True
 L1_NEW = True
 ORDER = "L0first"
-SPLIT = (76, 112)
+SPLIT = (60, 96)
+PE_Q = 32
 HEAD_SPLITS = ((48, 72), (64, 96))
 Q1S = 24
 RAW_BUFS = 8
@@ -40,6 +41,8 @@ def tile_head_t_kernel(tc, f0, f1, f2, w0, b0, w1, b1, w2, b2, anchors, out):
 
         ident = const.tile([P, P], F32, name="ident")
         make_identity(nc, ident[:])
+        ident_b = const.tile([P, P], BF16, name="ident_b")
+        nc.vector.tensor_copy(out=ident_b[:], in_=ident[:])
         ones = const.tile([P, P], BF16, name="ones")
         nc.vector.memset(ones[:], 1.0)
         crow = const.tile([P, 800], BF16, name="crow")
@@ -183,6 +186,7 @@ def tile_head_t_kernel(tc, f0, f1, f2, w0, b0, w1, b1, w2, b2, anchors, out):
         def make_l0(n, split):
             st = {}
             qs, qg = split
+            on_tensor = split == SPLIT
 
             def load():
                 st["raw"] = rawp.tile([P, 4096], BF16, tag="raw", name="raw")
@@ -203,6 +207,17 @@ def tile_head_t_kernel(tc, f0, f1, f2, w0, b0, w1, b1, w2, b2, anchors, out):
                 for th in range(2):
                     ts = slice(4 * th, 4 * th + 4)
                     pool_copy(dst_c[:, qs:qg, ts, :], src_c[:, qs:qg, ts, :])
+                if on_tensor:
+                    src_t = st["raw"][:].rearrange("p (j q t) -> p t q j", j=4, q=128, t=8)
+                    dst_t = st["grp"][:].rearrange("p (t x) -> p t x", t=8)
+                    rps = psum.tile([P, 1024], BF16, tag="bank", name="rps")
+                    for th in range(2):
+                        nc.tensor.matmul(
+                            out=rps[:, 512 * th : 512 * (th + 1)], lhsT=ident_b[:],
+                            rhs=src_t[:, 4 * th : 4 * th + 4, qg:128, :], start=True, stop=True,
+                        )
+                    nc.scalar.copy(out=dst_t[:, :, 4 * qg : 512], in_=rps[:].rearrange("p (t x) -> p t x", t=8))
+                    return
                 for th in range(2):
                     ts = slice(4 * th, 4 * th + 4)
                     if FORM_A:

@@ -15,16 +15,17 @@ ALU = mybir.AluOpType
 P = 128
 FLOPS = 2 * 256 * (512 * 12 * 1024 + 512 * 12 * 256 + 1024 * 12 * 64)
 
-FORM_A = True
-L1_NEW = True
-ORDER = "L0first"
-SPLIT = (60, 96)
-PE_Q = 32
+UNITS = [(0, n) for n in range(6)] + [(1, u) for u in range(3)] + [(2, h) for h in range(2)] + [(0, n) for n in range(6, 12)]
 HEAD_SPLITS = ((48, 72), (64, 96))
-Q1S = 24
-RAW_BUFS = 8
-OUT_BUFS = 8
-W_STEPS = (6, 9)
+SPLIT = (56, 96)
+L1_S = 64
+OUT_BUFS = 5
+LOADS = (
+    (-1, "w", 0), (-1, "f0", 0, 1), (-1, "f0", 1, 2), (-1, "f0", 2, 3), (-1, "f0", 3, 6), (-1, "w", 1), (-1, "f1",), (-1, "w", 2), (-1, "f2",),
+    (2, "f0", 6, 9), (4, "f0", 9, 12),
+)
+W_PREP = ((1, 3), (2, 5))
+W_SCALAR = (2,)
 
 
 def tile_head_t_kernel(tc, f0, f1, f2, w0, b0, w1, b1, w2, b2, anchors, out):
@@ -32,12 +33,13 @@ def tile_head_t_kernel(tc, f0, f1, f2, w0, b0, w1, b1, w2, b2, anchors, out):
     with ExitStack() as ctx:
         ctx.enter_context(tc.manual_schedule())
         const = ctx.enter_context(tc.tile_pool(name="const", bufs=1))
-        rawp = ctx.enter_context(tc.tile_pool(name="rawp", bufs=RAW_BUFS))
+        rawp = ctx.enter_context(tc.tile_pool(name="rawp", bufs=4))
         grpp = ctx.enter_context(tc.tile_pool(name="grpp", bufs=2))
         codp = ctx.enter_context(tc.tile_pool(name="codp", bufs=3))
         outp = ctx.enter_context(tc.tile_pool(name="outp", bufs=OUT_BUFS))
         smallp = ctx.enter_context(tc.tile_pool(name="smallp", bufs=3))
-        psum = ctx.enter_context(tc.psum_pool(name="psum", bufs=8))
+        psum = ctx.enter_context(tc.psum_pool(name="psum", bufs=6))
+        psumr = ctx.enter_context(tc.psum_pool(name="psumr", bufs=2))
 
         ident = const.tile([P, P], F32, name="ident")
         make_identity(nc, ident[:])
@@ -61,59 +63,79 @@ def tile_head_t_kernel(tc, f0, f1, f2, w0, b0, w1, b1, w2, b2, anchors, out):
             nc.tensor.matmul(out=cps1[:, 256:288], lhsT=ones[:], rhs=crow[:, 768:800], start=True, stop=True)
             nc.vector.tensor_copy(out=cst[:, 0:512], in_=cps0[:])
             nc.vector.tensor_copy(out=cst[:, 512:800], in_=cps1[:, 0:288])
-            a0 = cst[:, 768:776].rearrange("p (a c) -> p a c", a=4).unsqueeze(2)
-            nc.gpsimd.tensor_copy(
-                out=ancx[0][:].rearrange("p (a t) c -> p a t c", a=4), in_=a0.to_broadcast([P, 4, 8, 2])
-            )
-            a1 = cst[:, 776:784].rearrange("p (a c) -> p a c", a=4).unsqueeze(2)
-            if L1_NEW:
+            for lvl, rep in ((0, 8), (1, 8), (2, 3)):
+                src = cst[:, 768 + 8 * lvl : 776 + 8 * lvl].rearrange("p (a c) -> p a c", a=4).unsqueeze(2)
                 nc.gpsimd.tensor_copy(
-                    out=ancx[1][:].rearrange("p (a t) c -> p a t c", a=4), in_=a1.to_broadcast([P, 4, 8, 2])
+                    out=ancx[lvl][:, 0 : 4 * rep, :].rearrange("p (a t) c -> p a t c", a=4),
+                    in_=src.to_broadcast([P, 4, rep, 2]),
                 )
-            else:
-                for n in range(4):
-                    nc.gpsimd.tensor_copy(
-                        out=ancx[1][:, 8 * n : 8 * n + 8, :].rearrange("p (a t) c -> p a t c", a=4),
-                        in_=a1.to_broadcast([P, 4, 2, 2]),
-                    )
-            a2 = cst[:, 784:792].unsqueeze(1)
-            nc.gpsimd.tensor_copy(
-                out=ancx[2][:, 0:12, :].rearrange("p (m a) c -> p m (a c)", m=3), in_=a2.to_broadcast([P, 3, 8])
-            )
 
         wts = {}
 
-        def load_w(lvl, w, K):
+        def load_w(lvl):
+            w, K = ((w0, 512), (w1, 512), (w2, 1024))[lvl]
             w_sb = const.tile([P, 2 * K], BF16, name="w_sb%d" % lvl)
             nc.sync.dma_start(
                 out=w_sb[:].rearrange("o (b k) -> o b k", b=2), in_=w.rearrange("(b o) k -> o b k", b=2)
             )
             wts[lvl] = (w_sb, K)
 
-        def prep_w_a(lvl, on_scalar):
+        def turn_w(lvl):
             w_sb, K = wts[lvl]
             passes = K // 512
             wc = const.tile([P, passes * 256], U32, name="wc%d" % lvl, align_bytes=64)
             ws = const.tile([P, passes * 256], U8, name="ws%d" % lvl, align_bytes=64)
             wg = const.tile([P, passes * 1024], BF16, name="wg%d" % lvl, align_bytes=64)
             words = w_sb[:].bitcast(F32).rearrange("o (b g m u) -> o b g u m", b=2, g=passes, m=128, u=2)
+            banks = []
             for g in range(passes):
-                xt = psum.tile([P, 512], F32, tag="bank", name="xt")
+                xt = psumr.tile([P, 512], F32, tag="rps", name="xt")
+                banks.append(xt)
                 for u in range(2):
                     for b in range(2):
                         c0 = u * 256 + b * 128
                         nc.tensor.transpose(xt[:, c0 : c0 + 128], words[:, b, g, u, :], ident[:])
+            wts[lvl] = (wc, ws, wg, banks)
+
+        def group_w(lvl, on_scalar):
+            wc, ws, wg, banks = wts[lvl]
+            for g, xt in enumerate(banks):
                 wgv = wg[:, g * 1024 : (g + 1) * 1024].bitcast(F32).rearrange("p (o u) -> p o u", u=2)
                 if on_scalar:
                     nc.scalar.copy(out=wgv, in_=xt[:].rearrange("p (u o) -> p o u", u=2))
                 else:
                     nc.vector.tensor_copy(out=wgv, in_=xt[:].rearrange("p (u o) -> p o u", u=2))
-            wts[lvl] = (wc, ws, wg)
 
-        def prep_w_b(lvl):
-            wc, ws, wg = wts[lvl]
+        def quant_w(lvl):
+            wc, ws, wg, banks = wts[lvl]
             nc.vector.quantize_mx(out=wc[:].bitcast(FP8X4), scales=ws[:], in_=wg[:])
             wts[lvl] = (wc, ws)
+
+        raws = {}
+
+        def load_f0(n0, n1):
+            if n0 % 3 == 0:
+                raws[n0 // 3] = rawp.tile([P, 12288], BF16, tag="raw", name="raw")
+            c0 = 4096 * (n0 % 3)
+            nc.sync.dma_start(
+                out=raws[n0 // 3][:, c0 : c0 + 4096 * (n1 - n0)].rearrange("p (n x) -> p n x", n=n1 - n0),
+                in_=f0[n0:n1].rearrange("n (p j) h w -> p n (j h w)", j=4),
+            )
+
+        def load_f1():
+            raws["f1"] = rawp.tile([P, 12288], BF16, tag="raw", name="raw")
+            nc.sync.dma_start(
+                out=raws["f1"][:].rearrange("p (n x) -> p n x", n=12),
+                in_=f1.rearrange("n (p j) h w -> p n (j h w)", j=4),
+            )
+
+        def load_f2():
+            raws["f2"] = rawp.tile([P, 6144], BF16, tag="raw", name="raw")
+            for g in range(2):
+                nc.sync.dma_start(
+                    out=raws["f2"][:, 3072 * g : 3072 * (g + 1)].rearrange("p (n x) -> p n x", n=12),
+                    in_=f2[:, 512 * g : 512 * (g + 1)].rearrange("n (p j) h w -> p n (j h w)", j=4),
+                )
 
         def pool_copy(dst, src):
             nc.gpsimd.tensor_scalar(out=dst, in0=src, scalar1=1.0, scalar2=0.0, op0=ALU.mult, op1=ALU.add)
@@ -130,20 +152,30 @@ def tile_head_t_kernel(tc, f0, f1, f2, w0, b0, w1, b1, w2, b2, anchors, out):
                 stop=stop,
             )
 
-        def small_s(st, rows):
-            rowsv = st["osb"][:, 0 : rows * 64].rearrange("p (r j) -> p r j", j=64)
+        def fields(ap, lo, hi):
+            return ap[:, :, lo:hi] if len(ap.shape) == 3 else ap[:, :, :, lo:hi]
+
+        def small_s(st):
+            rows = st["rows"]
+            d = list(rows.shape[1:-1])
+            n = d[0] * (d[1] if len(d) > 1 else 1)
             sg = smallp.tile([P, 32, 4], F32, tag="sg", name="sg")
             sq = smallp.tile([P, 32, 2], F32, tag="sq", name="sq")
-            nc.scalar.activation(out=sg[:, 0:rows, :], in_=rowsv[:, :, 0:4], func=ACT.Sigmoid)
-            nc.scalar.activation(out=rowsv[:, :, 0:2], in_=sg[:, 0:rows, 0:2], func=ACT.Copy, scale=2.0, bias=-0.5)
-            nc.scalar.activation(out=sq[:, 0:rows, :], in_=sg[:, 0:rows, 2:4], func=ACT.Square, scale=2.0)
-            st["sq"] = sq
+            sgv, sqv = sg[:, 0:n, :], sq[:, 0:n, :]
+            if len(d) > 1:
+                sgv = sgv.rearrange("p (a r) c -> p a r c", a=d[0])
+                sqv = sqv.rearrange("p (a r) c -> p a r c", a=d[0])
+            nc.scalar.activation(out=sgv, in_=fields(rows, 0, 4), func=ACT.Sigmoid)
+            nc.scalar.activation(out=fields(rows, 0, 2), in_=fields(sgv, 0, 2), func=ACT.Copy, scale=2.0, bias=-0.5)
+            nc.scalar.activation(out=sqv, in_=fields(sgv, 2, 4), func=ACT.Square, scale=2.0)
+            st["sq"] = (sqv, n, d)
 
-        def small_g(st, rows, lvl):
-            rowsv = st["osb"][:, 0 : rows * 64].rearrange("p (r j) -> p r j", j=64)
-            nc.gpsimd.tensor_tensor(
-                out=rowsv[:, :, 2:4], in0=st["sq"][:, 0:rows, :], in1=ancx[lvl][:, 0:rows, :], op=ALU.mult
-            )
+        def small_g(st, lvl):
+            sqv, n, d = st["sq"]
+            anc = ancx[lvl][:, 0:n, :]
+            if len(d) > 1:
+                anc = anc.rearrange("p (a r) c -> p a r c", a=d[0])
+            nc.gpsimd.tensor_tensor(out=fields(st["rows"], 2, 4), in0=sqv, in1=anc, op=ALU.mult)
 
         def bias_at(lvl):
             return (
@@ -164,7 +196,6 @@ def tile_head_t_kernel(tc, f0, f1, f2, w0, b0, w1, b1, w2, b2, anchors, out):
                 )
 
         def eight_tiles(st, lvl):
-            quant(st, 4096, ((0, 2048), (2048, 4096)))
             st["ps"] = []
             for b in range(4):
                 ps = psum.tile([P, 512], F32, tag="bank", name="acc")
@@ -172,12 +203,10 @@ def tile_head_t_kernel(tc, f0, f1, f2, w0, b0, w1, b1, w2, b2, anchors, out):
                     mx(ps[:, 256 * i : 256 * (i + 1)], st, (2 * b + i) * 128, lvl, 0, True, True)
                 st["ps"].append(ps)
 
-        def evac_rows8(st, lvl):
-            st["osb"] = outp.tile([P, 2048], F32, tag="osb", name="osb")
-            ov = st["osb"][:].rearrange("p (a t j) -> p a t j", a=4, t=8, j=64)
+        def evac_banks(st, lvl, view):
             for b in range(4):
                 nc.vector.tensor_tensor(
-                    out=ov[:, :, 2 * b : 2 * b + 2, :],
+                    out=view(b),
                     in0=st["ps"][b][:].rearrange("p (t a j) -> p a t j", t=2, a=4, j=64),
                     in1=bias_at(lvl),
                     op=ALU.add,
@@ -188,42 +217,45 @@ def tile_head_t_kernel(tc, f0, f1, f2, w0, b0, w1, b1, w2, b2, anchors, out):
             qs, qg = split
             on_tensor = split == SPLIT
 
-            def load():
-                st["raw"] = rawp.tile([P, 4096], BF16, tag="raw", name="raw")
-                nc.sync.dma_start(out=st["raw"][:], in_=f0[n].rearrange("(p j) h w -> p (j h w)", j=4))
+            def turn():
+                if not on_tensor:
+                    return
+                raw = raws[n // 3][:, 4096 * (n % 3) : 4096 * (n % 3 + 1)]
+                src_t = raw.rearrange("p (j q t) -> p t q j", j=4, q=128, t=8)
+                st["rps"] = psumr.tile([P, 1024], BF16, tag="rps", name="rps")
+                for th in range(2):
+                    nc.tensor.matmul(
+                        out=st["rps"][:, 512 * th : 512 * (th + 1)], lhsT=ident_b[:],
+                        rhs=src_t[:, 4 * th : 4 * th + 4, qg:128, :], start=True, stop=True,
+                    )
 
             def regroup():
                 st["grp"] = grpp.tile([P, 4096], BF16, tag="grp", name="grp", align_bytes=64)
-                src_c = st["raw"][:].rearrange("p (j q t) -> p q t j", j=4, q=128, t=8)
+                raw = raws[n // 3][:, 4096 * (n % 3) : 4096 * (n % 3 + 1)]
+                src_c = raw.rearrange("p (j q t) -> p q t j", j=4, q=128, t=8)
                 dst_c = st["grp"][:].rearrange("p (t q j) -> p q t j", t=8, q=128, j=4)
-                src_a = st["raw"][:].rearrange("p (j q t) -> p q j t", j=4, q=128, t=8)
+                src_a = raw.rearrange("p (j q t) -> p q j t", j=4, q=128, t=8)
                 dst_a = st["grp"][:].rearrange("p (t q j) -> p q j t", t=8, q=128, j=4)
-                for th in range(2):
-                    ts = slice(4 * th, 4 * th + 4)
-                    if FORM_A:
-                        nc.scalar.copy(out=dst_a[:, 0:qs, :, ts], in_=src_a[:, 0:qs, :, ts])
-                    else:
-                        nc.scalar.copy(out=dst_c[:, 0:qs, ts, :], in_=src_c[:, 0:qs, ts, :])
-                for th in range(2):
-                    ts = slice(4 * th, 4 * th + 4)
+                halves = (slice(0, 4), slice(4, 8))
+                if on_tensor:
+                    nc.scalar.copy(
+                        out=st["grp"][:].rearrange("p (t x) -> p t x", t=8)[:, :, 4 * qg : 512],
+                        in_=st["rps"][:].rearrange("p (t x) -> p t x", t=8),
+                    )
+                for ts in halves:
+                    nc.scalar.copy(out=dst_a[:, 0:qs, :, ts], in_=src_a[:, 0:qs, :, ts])
+                for ts in halves:
                     pool_copy(dst_c[:, qs:qg, ts, :], src_c[:, qs:qg, ts, :])
                 if on_tensor:
-                    src_t = st["raw"][:].rearrange("p (j q t) -> p t q j", j=4, q=128, t=8)
-                    dst_t = st["grp"][:].rearrange("p (t x) -> p t x", t=8)
-                    rps = psum.tile([P, 1024], BF16, tag="bank", name="rps")
-                    for th in range(2):
-                        nc.tensor.matmul(
-                            out=rps[:, 512 * th : 512 * (th + 1)], lhsT=ident_b[:],
-                            rhs=src_t[:, 4 * th : 4 * th + 4, qg:128, :], start=True, stop=True,
-                        )
-                    nc.scalar.copy(out=dst_t[:, :, 4 * qg : 512], in_=rps[:].rearrange("p (t x) -> p t x", t=8))
                     return
-                for th in range(2):
-                    ts = slice(4 * th, 4 * th + 4)
-                    if FORM_A:
-                        nc.vector.tensor_copy(out=dst_a[:, qg:128, :, ts], in_=src_a[:, qg:128, :, ts])
-                    else:
-                        nc.vector.tensor_copy(out=dst_c[:, qg:128, ts, :], in_=src_c[:, qg:128, ts, :])
+                for ts in halves:
+                    nc.vector.tensor_copy(out=dst_a[:, qg:128, :, ts], in_=src_a[:, qg:128, :, ts])
+
+            def evac():
+                st["osb"] = outp.tile([P, 2048], F32, tag="osb", name="osb")
+                ov = st["osb"][:].rearrange("p (a t j) -> p a t j", a=4, t=8, j=64)
+                evac_banks(st, 0, lambda b: ov[:, :, 2 * b : 2 * b + 2, :])
+                st["rows"] = st["osb"][:].rearrange("p (r j) -> p r j", j=64)
 
             def store():
                 nc.sync.dma_start(
@@ -232,105 +264,71 @@ def tile_head_t_kernel(tc, f0, f1, f2, w0, b0, w1, b1, w2, b2, anchors, out):
                 )
 
             return {
-                "load": load, "regroup": regroup, "quant_mm": lambda: eight_tiles(st, 0),
-                "evac": lambda: evac_rows8(st, 0), "small_s": lambda: small_s(st, 32),
-                "small_g": lambda: small_g(st, 32, 0), "store": store,
+                "turn": turn, "regroup": regroup, "mm": lambda: eight_tiles(st, 0), "quant": lambda: quant(st, 4096, ((0, 2048), (2048, 4096))), "evac": evac,
+                "small_s": lambda: small_s(st), "small_g": lambda: small_g(st, 0), "store": store,
             }
 
-        def make_l1(u, split_load):
+        shared = {}
+
+        def make_l1(u):
             st = {}
 
-            def load():
-                st["raw"] = rawp.tile([P, 4096], BF16, tag="raw", name="raw")
-                if split_load:
-                    for n in range(4):
-                        nc.sync.dma_start(
-                            out=st["raw"][:, 1024 * n : 1024 * (n + 1)],
-                            in_=f1[4 * u + n].rearrange("(p j) h w -> p (j h w)", j=4),
+            def regroup():
+                st["grp"] = grpp.tile([P, 4096], BF16, tag="grp", name="grp", align_bytes=64)
+                for i in range(4):
+                    raw = raws["f1"][:, 1024 * (4 * u + i) : 1024 * (4 * u + i + 1)]
+                    grp = st["grp"][:, 1024 * i : 1024 * (i + 1)]
+                    src = raw.rearrange("p (j v l t) -> p v j l t", j=4, v=64, l=2, t=2)
+                    dst = grp.rearrange("p (t v l j) -> p v j l t", t=2, v=64, l=2, j=4)
+                    if i == 3:
+                        pool_copy(
+                            grp.rearrange("p (t q j) -> p q t j", t=2, q=128, j=4),
+                            raw.rearrange("p (j q t) -> p q t j", j=4, q=128, t=2),
                         )
-                else:
-                    nc.sync.dma_start(
-                        out=st["raw"][:].rearrange("p (n x) -> p n x", n=4),
-                        in_=f1[4 * u : 4 * u + 4].rearrange("n (p j) h w -> p n (j h w)", j=4),
-                    )
-
-            def regroup_new():
-                st["grp"] = grpp.tile([P, 4096], BF16, tag="grp", name="grp", align_bytes=64)
-                src = st["raw"][:].rearrange("p (i q t) -> p q i t", i=16, q=32, t=8)
-                dst = st["grp"][:].rearrange("p (t q i) -> p q i t", t=8, q=32, i=16)
-                for th in range(2):
-                    ts = slice(4 * th, 4 * th + 4)
-                    nc.scalar.copy(out=dst[:, 0:Q1S, :, ts], in_=src[:, 0:Q1S, :, ts])
-                for th in range(2):
-                    ts = slice(4 * th, 4 * th + 4)
-                    pool_copy(dst[:, Q1S:32, :, ts], src[:, Q1S:32, :, ts])
-
-            def regroup_old():
-                st["grp"] = grpp.tile([P, 4096], BF16, tag="grp", name="grp", align_bytes=64)
-                for n in range(4):
-                    src = st["raw"][:, 1024 * n : 1024 * (n + 1)].rearrange("p (j q t) -> p q t j", j=4, q=128, t=2)
-                    dst = st["grp"][:, 1024 * n : 1024 * (n + 1)].rearrange("p (t q j) -> p q t j", t=2, q=128, j=4)
-                    if n < 2:
-                        nc.scalar.copy(out=dst, in_=src)
-                    elif n == 2:
-                        pool_copy(dst, src)
+                    elif i == 2:
+                        v = L1_S // 2
+                        nc.scalar.copy(out=dst[:, 0:v], in_=src[:, 0:v])
+                        nc.vector.tensor_copy(out=dst[:, v:64], in_=src[:, v:64])
                     else:
-                        nc.scalar.copy(out=dst[:, 0:64], in_=src[:, 0:64])
-                        nc.vector.tensor_copy(out=dst[:, 64:128], in_=src[:, 64:128])
+                        nc.scalar.copy(out=dst, in_=src)
 
-            def evac_old():
-                st["osb"] = outp.tile([P, 2048], F32, tag="osb", name="osb")
-                for n in range(4):
-                    nc.vector.tensor_tensor(
-                        out=st["osb"][:, 512 * n : 512 * (n + 1)].rearrange("p (a t j) -> p a t j", a=4, t=2, j=64),
-                        in0=st["ps"][n][:].rearrange("p (t a j) -> p a t j", t=2, a=4, j=64),
-                        in1=bias_at(1),
-                        op=ALU.add,
-                    )
+            def evac():
+                if u == 0:
+                    shared["o1"] = const.tile([P, 6144], F32, name="o1")
+                ov = shared["o1"][:].rearrange("p (a n t j) -> p a n t j", a=4, n=12, t=2, j=64)
+                evac_banks(st, 1, lambda b: ov[:, :, 4 * u + b, :, :])
+                st["rows"] = shared["o1"][:].rearrange("p (a r j) -> p a r j", a=4, r=24, j=64)[:, :, 8 * u : 8 * u + 8, :]
 
             def store():
-                for n in range(4):
-                    if L1_NEW:
-                        nc.sync.dma_start(
-                            out=out[4 * u + n, 4096:5120, :].rearrange("(a q t) j -> q a (t j)", a=4, q=32, t=8),
-                            in_=st["osb"][n:128:4, :].rearrange("p (a x) -> p a x", a=4),
-                        )
-                    else:
-                        nc.sync.dma_start(
-                            out=out[4 * u + n, 4096:5120, :].rearrange("(a q t) j -> q a (t j)", a=4, q=128, t=2),
-                            in_=st["osb"][:, 512 * n : 512 * (n + 1)].rearrange("p (a x) -> p a x", a=4),
-                        )
+                if u < 2:
+                    return
+                for a in range(4):
+                    nc.sync.dma_start(
+                        out=out[:, 4096 + 256 * a : 4096 + 256 * (a + 1), :].rearrange("n (q t) j -> q n (t j)", q=128, t=2),
+                        in_=shared["o1"][:, 1536 * a : 1536 * (a + 1)].rearrange("p (n x) -> p n x", n=12),
+                    )
 
             return {
-                "load": load, "regroup": regroup_new if L1_NEW else regroup_old,
-                "quant_mm": lambda: eight_tiles(st, 1),
-                "evac": (lambda: evac_rows8(st, 1)) if L1_NEW else evac_old,
-                "small_s": lambda: small_s(st, 32), "small_g": lambda: small_g(st, 32, 1), "store": store,
+                "turn": lambda: None, "regroup": regroup, "mm": lambda: eight_tiles(st, 1), "quant": lambda: quant(st, 4096, ((0, 2048), (2048, 4096))), "evac": evac,
+                "small_s": lambda: small_s(st), "small_g": lambda: small_g(st, 1), "store": store,
             }
 
         def make_l2(h):
             st = {}
 
-            def load():
-                st["raw"] = rawp.tile([P, 3072], BF16, tag="raw", name="raw")
-                nc.sync.dma_start(
-                    out=st["raw"][:].rearrange("p (x y) -> p x y", x=12),
-                    in_=f2[6 * h : 6 * h + 6].rearrange("n (g p j) h w -> p (n g) (j h w)", g=2, p=128, j=4),
-                )
-
             def regroup():
                 st["grp"] = grpp.tile([P, 3072], BF16, tag="grp", name="grp", align_bytes=64)
-                src = st["raw"][:].rearrange("p (n g j s) -> p g n s j", n=6, g=2, j=4, s=64)
-                dst = st["grp"][:].rearrange("p (g n s j) -> p g n s j", g=2, n=6, s=64, j=4)
+                src = raws["f2"][:].rearrange("p (g m i v r) -> p g m v i r", g=2, m=6, i=8, v=16, r=4)[:, :, 3 * h : 3 * h + 3]
+                dst = st["grp"][:].rearrange("p (g m v r i) -> p g m v i r", g=2, m=3, v=16, r=4, i=8)
                 for g in range(2):
-                    nc.scalar.copy(out=dst[:, g, 0:3], in_=src[:, g, 0:3])
+                    nc.scalar.copy(out=dst[:, g, 0], in_=src[:, g, 0])
+                    nc.scalar.copy(out=dst[:, g, 1, 0:8], in_=src[:, g, 1, 0:8])
                 for g in range(2):
-                    pool_copy(dst[:, g, 3:5], src[:, g, 3:5])
+                    pool_copy(dst[:, g, 2], src[:, g, 2])
                 for g in range(2):
-                    nc.vector.tensor_copy(out=dst[:, g, 5:6], in_=src[:, g, 5:6])
+                    nc.vector.tensor_copy(out=dst[:, g, 1, 8:16], in_=src[:, g, 1, 8:16])
 
-            def quant_mm():
-                quant(st, 3072, ((0, 2048), (2048, 3072)))
+            def mm():
                 st["ps"] = []
                 for b in range(2):
                     ps = psum.tile([P, 512], F32, tag="bank", name="acc")
@@ -341,80 +339,92 @@ def tile_head_t_kernel(tc, f0, f1, f2, w0, b0, w1, b1, w2, b2, anchors, out):
                     st["ps"].append(ps)
 
             def evac():
-                st["osb"] = outp.tile([P, 768], F32, tag="osb", name="osb")
+                if h == 0:
+                    shared["o2"] = const.tile([P, 1536], F32, name="o2")
+                ov = shared["o2"][:].rearrange("p (a m j) -> p a m j", a=4, m=6, j=64)
+                bias = cst[:, 512:768].rearrange("p (a j) -> p a j", a=4)
                 nc.vector.tensor_tensor(
-                    out=st["osb"][:, 0:512].rearrange("p (m x) -> p m x", m=2),
-                    in0=st["ps"][0][:].rearrange("p (m x) -> p m x", m=2),
-                    in1=cst[:, 512:768].unsqueeze(1).to_broadcast([P, 2, 256]),
+                    out=ov[:, :, 3 * h : 3 * h + 2, :],
+                    in0=st["ps"][0][:].rearrange("p (m a j) -> p a m j", m=2, a=4),
+                    in1=bias.unsqueeze(2).to_broadcast([P, 4, 2, 64]),
                     op=ALU.add,
                 )
                 nc.vector.tensor_tensor(
-                    out=st["osb"][:, 512:768], in0=st["ps"][1][:, 0:256], in1=cst[:, 512:768], op=ALU.add
+                    out=ov[:, :, 3 * h + 2, :],
+                    in0=st["ps"][1][:, 0:256].rearrange("p (a j) -> p a j", a=4),
+                    in1=bias,
+                    op=ALU.add,
                 )
+                st["rows"] = ov[:, :, 3 * h : 3 * h + 3, :]
 
             def store():
-                for m in range(3):
-                    for n2 in range(2):
+                if h < 1:
+                    return
+                o = out[:, 5120:5376, :].rearrange("(m b) (a s) j -> b a s m j", b=2, a=4)
+                for b in range(2):
+                    for a in range(4):
                         nc.sync.dma_start(
-                            out=out[6 * h + 2 * m + n2, 5120:5376, :].rearrange("(a s) j -> s a j", a=4),
-                            in_=st["osb"][64 * n2 : 64 * n2 + 64, 256 * m : 256 * (m + 1)].rearrange(
-                                "p (a j) -> p a j", a=4
-                            ),
+                            out=o[b, a],
+                            in_=shared["o2"][b:128:2, 384 * a : 384 * (a + 1)].rearrange("p (m j) -> p m j", m=6),
                         )
 
             return {
-                "load": load, "regroup": regroup, "quant_mm": quant_mm, "evac": evac,
-                "small_s": lambda: small_s(st, 12), "small_g": lambda: small_g(st, 12, 2), "store": store,
+                "turn": lambda: None, "regroup": regroup, "mm": mm, "quant": lambda: quant(st, 3072, ((0, 2048), (2048, 3072))), "evac": evac,
+                "small_s": lambda: small_s(st), "small_g": lambda: small_g(st, 2), "store": store,
             }
 
-        wsrc = {0: (w0, 512), 1: (w1, 512), 2: (w2, 1024)}
-        if ORDER == "L1first":
-            units = [make_l1(u, u < 2) for u in range(3)] + [make_l0(n, SPLIT) for n in range(12)]
-            lv = (1, 0, 2)
-        else:
-            units = [make_l0(n, HEAD_SPLITS[n] if n < len(HEAD_SPLITS) else SPLIT) for n in range(12)]
-            units = units + [make_l1(u, False) for u in range(3)]
-            lv = (0, 1, 2)
-        units = units + [make_l2(h) for h in range(2)]
+        units = []
+        for lvl, i in UNITS:
+            if lvl == 0:
+                units.append(make_l0(i, HEAD_SPLITS[i] if i < len(HEAD_SPLITS) else SPLIT))
+            else:
+                units.append(make_l1(i) if lvl == 1 else make_l2(i))
         N = len(units)
 
-        load_w(lv[0], wsrc[lv[0]][0], wsrc[lv[0]][1])
-        units[0]["load"]()
-        units[1]["load"]()
-        load_w(lv[1], wsrc[lv[1]][0], wsrc[lv[1]][1])
-        units[2]["load"]()
-        units[3]["load"]()
-        load_w(lv[2], wsrc[lv[2]][0], wsrc[lv[2]][1])
-        for i in range(4, RAW_BUFS):
-            units[i]["load"]()
-        prep_w_a(lv[0], False)
-        prep_w_b(lv[0])
+        def issue(step):
+            for ld in LOADS:
+                if ld[0] == step:
+                    if ld[1] == "w":
+                        load_w(ld[2])
+                    elif ld[1] == "f0":
+                        load_f0(ld[2], ld[3])
+                    elif ld[1] == "f1":
+                        load_f1()
+                    else:
+                        load_f2()
+
+        issue(-1)
+        turn_w(0)
+        group_w(0, False)
+        quant_w(0)
         units[0]["regroup"]()
-        units[RAW_BUFS]["load"]()
         spread_constants()
-        units[0]["quant_mm"]()
+        units[0]["quant"]()
+        units[0]["mm"]()
         units[1]["regroup"]()
-        units[RAW_BUFS + 1]["load"]()
+        units[2]["turn"]()
 
         for k in range(N + 2):
             if 0 <= k - 2 < N:
                 units[k - 2]["small_s"]()
             if 0 < k < N:
-                units[k]["quant_mm"]()
+                units[k]["quant"]()
             if 0 <= k - 1 < N:
                 units[k - 1]["evac"]()
+            if 0 < k < N:
+                units[k]["mm"]()
+            if k + 3 < N:
+                units[k + 3]["turn"]()
             if k + 2 < N:
                 units[k + 2]["regroup"]()
-            if k + 2 + RAW_BUFS < N:
-                units[k + 2 + RAW_BUFS]["load"]()
             if 0 <= k - 2 < N:
                 units[k - 2]["small_g"]()
                 units[k - 2]["store"]()
-            if k == W_STEPS[0]:
-                prep_w_a(lv[1], W_STEPS[0] > 2)
-            if k == W_STEPS[0] + 1:
-                prep_w_b(lv[1])
-            if k == W_STEPS[1]:
-                prep_w_a(lv[2], True)
-            if k == W_STEPS[1] + 1:
-                prep_w_b(lv[2])
+            issue(k)
+            for lvl, first in W_PREP:
+                if k == first:
+                    turn_w(lvl)
+                elif k == first + 1:
+                    group_w(lvl, lvl in W_SCALAR)
+                elif k == first + 2:
+                    quant_w(lvl)

@@ -16,13 +16,14 @@ P = 128
 FLOPS = 2 * 256 * (512 * 12 * 1024 + 512 * 12 * 256 + 1024 * 12 * 64)
 
 UNITS = [(0, n) for n in range(6)] + [(1, u) for u in range(3)] + [(2, h) for h in range(2)] + [(0, n) for n in range(6, 12)]
-HEAD_SPLITS = ((48, 72), (64, 96))
+HEAD_SPLITS = ((44, 44), (60, 60))
 SPLIT = (56, 96)
+PLAIN = (76, 112)
+TENSOR_FROM = 4
 L1_S = 64
 OUT_BUFS = 5
 LOADS = (
-    (-1, "w", 0), (-1, "f0", 0, 1), (-1, "f0", 1, 2), (-1, "f0", 2, 3), (-1, "f0", 3, 6), (-1, "w", 1), (-1, "f1",), (-1, "w", 2), (-1, "f2",),
-    (2, "f0", 6, 9), (4, "f0", 9, 12),
+    (-1, "w", 0), (-1, "f0", 0, 1), (-1, "f0", 1, 2), (-1, "f0", 2, 3), (-1, "f0", 3, 4), (-1, "f0", 4, 6), (-1, "w", 1), (-1, "f1",), (-1, "w", 2), (-1, "f0", 6, 9), (3, "f2",), (6, "f0", 9, 12),
 )
 W_PREP = ((1, 3), (2, 5))
 W_SCALAR = (2,)
@@ -34,6 +35,8 @@ def tile_head_t_kernel(tc, f0, f1, f2, w0, b0, w1, b1, w2, b2, anchors, out):
         ctx.enter_context(tc.manual_schedule())
         const = ctx.enter_context(tc.tile_pool(name="const", bufs=1))
         rawp = ctx.enter_context(tc.tile_pool(name="rawp", bufs=4))
+        midp = ctx.enter_context(tc.tile_pool(name="midp", bufs=1))
+        bigp = ctx.enter_context(tc.tile_pool(name="bigp", bufs=2))
         grpp = ctx.enter_context(tc.tile_pool(name="grpp", bufs=2))
         codp = ctx.enter_context(tc.tile_pool(name="codp", bufs=3))
         outp = ctx.enter_context(tc.tile_pool(name="outp", bufs=OUT_BUFS))
@@ -61,8 +64,13 @@ def tile_head_t_kernel(tc, f0, f1, f2, w0, b0, w1, b1, w2, b2, anchors, out):
             cps1 = psum.tile([P, 512], F32, tag="bank", name="cps1")
             nc.tensor.matmul(out=cps1[:, 0:256], lhsT=ones[:], rhs=crow[:, 512:768], start=True, stop=True)
             nc.tensor.matmul(out=cps1[:, 256:288], lhsT=ones[:], rhs=crow[:, 768:800], start=True, stop=True)
+            return cps0, cps1
+
+        def keep_constants(cps0, cps1):
             nc.vector.tensor_copy(out=cst[:, 0:512], in_=cps0[:])
             nc.vector.tensor_copy(out=cst[:, 512:800], in_=cps1[:, 0:288])
+
+        def spread_anchors():
             for lvl, rep in ((0, 8), (1, 8), (2, 3)):
                 src = cst[:, 768 + 8 * lvl : 776 + 8 * lvl].rearrange("p (a c) -> p a c", a=4).unsqueeze(2)
                 nc.gpsimd.tensor_copy(
@@ -114,23 +122,29 @@ def tile_head_t_kernel(tc, f0, f1, f2, w0, b0, w1, b1, w2, b2, anchors, out):
         raws = {}
 
         def load_f0(n0, n1):
-            if n0 % 3 == 0:
-                raws[n0 // 3] = rawp.tile([P, 12288], BF16, tag="raw", name="raw")
-            c0 = 4096 * (n0 % 3)
+            width = 4096 * (n1 - n0)
+            if n1 - n0 == 1:
+                tile = rawp.tile([P, width], BF16, tag="raw", name="raw")
+            elif n1 - n0 == 2:
+                tile = midp.tile([P, width], BF16, tag="mid", name="mid")
+            else:
+                tile = bigp.tile([P, width], BF16, tag="big", name="big")
+            for n in range(n0, n1):
+                raws[n] = (tile, 4096 * (n - n0))
             nc.sync.dma_start(
-                out=raws[n0 // 3][:, c0 : c0 + 4096 * (n1 - n0)].rearrange("p (n x) -> p n x", n=n1 - n0),
+                out=tile[:].rearrange("p (n x) -> p n x", n=n1 - n0),
                 in_=f0[n0:n1].rearrange("n (p j) h w -> p n (j h w)", j=4),
             )
 
         def load_f1():
-            raws["f1"] = rawp.tile([P, 12288], BF16, tag="raw", name="raw")
+            raws["f1"] = bigp.tile([P, 12288], BF16, tag="big", name="big")
             nc.sync.dma_start(
                 out=raws["f1"][:].rearrange("p (n x) -> p n x", n=12),
                 in_=f1.rearrange("n (p j) h w -> p n (j h w)", j=4),
             )
 
         def load_f2():
-            raws["f2"] = rawp.tile([P, 6144], BF16, tag="raw", name="raw")
+            raws["f2"] = midp.tile([P, 6144], BF16, tag="mid", name="mid")
             for g in range(2):
                 nc.sync.dma_start(
                     out=raws["f2"][:, 3072 * g : 3072 * (g + 1)].rearrange("p (n x) -> p n x", n=12),
@@ -215,12 +229,13 @@ def tile_head_t_kernel(tc, f0, f1, f2, w0, b0, w1, b1, w2, b2, anchors, out):
         def make_l0(n, split):
             st = {}
             qs, qg = split
-            on_tensor = split == SPLIT
+            on_tensor = n >= TENSOR_FROM
 
             def turn():
                 if not on_tensor:
                     return
-                raw = raws[n // 3][:, 4096 * (n % 3) : 4096 * (n % 3 + 1)]
+                tile, c0 = raws[n]
+                raw = tile[:, c0 : c0 + 4096]
                 src_t = raw.rearrange("p (j q t) -> p t q j", j=4, q=128, t=8)
                 st["rps"] = psumr.tile([P, 1024], BF16, tag="rps", name="rps")
                 for th in range(2):
@@ -231,7 +246,8 @@ def tile_head_t_kernel(tc, f0, f1, f2, w0, b0, w1, b1, w2, b2, anchors, out):
 
             def regroup():
                 st["grp"] = grpp.tile([P, 4096], BF16, tag="grp", name="grp", align_bytes=64)
-                raw = raws[n // 3][:, 4096 * (n % 3) : 4096 * (n % 3 + 1)]
+                tile, c0 = raws[n]
+                raw = tile[:, c0 : c0 + 4096]
                 src_c = raw.rearrange("p (j q t) -> p q t j", j=4, q=128, t=8)
                 dst_c = st["grp"][:].rearrange("p (t q j) -> p q t j", t=8, q=128, j=4)
                 src_a = raw.rearrange("p (j q t) -> p q j t", j=4, q=128, t=8)
@@ -244,7 +260,7 @@ def tile_head_t_kernel(tc, f0, f1, f2, w0, b0, w1, b1, w2, b2, anchors, out):
                     )
                 for ts in halves:
                     nc.scalar.copy(out=dst_a[:, 0:qs, :, ts], in_=src_a[:, 0:qs, :, ts])
-                for ts in halves:
+                for ts in halves if qg > qs else ():
                     pool_copy(dst_c[:, qs:qg, ts, :], src_c[:, qs:qg, ts, :])
                 if on_tensor:
                     return
@@ -376,7 +392,7 @@ def tile_head_t_kernel(tc, f0, f1, f2, w0, b0, w1, b1, w2, b2, anchors, out):
         units = []
         for lvl, i in UNITS:
             if lvl == 0:
-                units.append(make_l0(i, HEAD_SPLITS[i] if i < len(HEAD_SPLITS) else SPLIT))
+                units.append(make_l0(i, HEAD_SPLITS[i] if i < len(HEAD_SPLITS) else PLAIN if i < TENSOR_FROM else SPLIT))
             else:
                 units.append(make_l1(i) if lvl == 1 else make_l2(i))
         N = len(units)
@@ -398,10 +414,12 @@ def tile_head_t_kernel(tc, f0, f1, f2, w0, b0, w1, b1, w2, b2, anchors, out):
         group_w(0, False)
         quant_w(0)
         units[0]["regroup"]()
-        spread_constants()
+        spread = spread_constants()
         units[0]["quant"]()
+        keep_constants(spread[0], spread[1])
         units[0]["mm"]()
         units[1]["regroup"]()
+        spread_anchors()
         units[2]["turn"]()
 
         for k in range(N + 2):

@@ -15,7 +15,7 @@ ALU = mybir.AluOpType
 P = 128
 FLOPS = 2 * 256 * (512 * 12 * 1024 + 512 * 12 * 256 + 1024 * 12 * 64)
 
-UNITS = [(0, n) for n in range(6)] + [(1, u) for u in range(3)] + [(2, h) for h in range(2)] + [(0, n) for n in range(6, 12)]
+UNITS = [(0, n) for n in range(6)] + [(1, u) for u in range(3)] + [(0, n) for n in range(6, 9)] + [(2, h) for h in range(2)] + [(0, n) for n in range(9, 12)]
 HEAD_SPLITS = ((44, 44), (60, 60))
 SPLIT = (56, 96)
 PLAIN = (76, 112)
@@ -25,7 +25,7 @@ OUT_BUFS = 5
 LOADS = (
     (-1, "w", 0), (-1, "f0", 0, 1), (-1, "f0", 1, 2), (-1, "f0", 2, 3), (-1, "f0", 3, 4), (-1, "f0", 4, 6), (-1, "w", 1), (-1, "f1",), (-1, "w", 2), (-1, "f0", 6, 9), (3, "f2",), (6, "f0", 9, 12),
 )
-W_PREP = ((1, 3), (2, 5))
+W_PREP = ((1, 3), (2, 8))
 W_SCALAR = (2,)
 
 
@@ -44,17 +44,16 @@ def tile_head_t_kernel(tc, f0, f1, f2, w0, b0, w1, b1, w2, b2, anchors, out):
         psum = ctx.enter_context(tc.psum_pool(name="psum", bufs=6))
         psumr = ctx.enter_context(tc.psum_pool(name="psumr", bufs=2))
 
-        ident = const.tile([P, P], F32, name="ident")
-        make_identity(nc, ident[:])
-        ident_b = const.tile([P, P], BF16, name="ident_b")
-        nc.vector.tensor_copy(out=ident_b[:], in_=ident[:])
-        ones = const.tile([P, P], BF16, name="ones")
-        nc.vector.memset(ones[:], 1.0)
         crow = const.tile([P, 800], BF16, name="crow")
         nc.vector.memset(crow[:].bitcast(I32), 0)
         for i, b in enumerate((b0, b1, b2)):
             nc.scalar.dma_start(out=crow[0:1, 256 * i : 256 * (i + 1)], in_=b.unsqueeze(0))
         nc.scalar.dma_start(out=crow[0:1, 768:792], in_=anchors.rearrange("l a c -> (l a c)").unsqueeze(0))
+        ident = const.tile([P, P], F32, name="ident")
+        make_identity(nc, ident[:])
+        ones = const.tile([P, P], BF16, name="ones")
+        nc.vector.memset(ones[:], 1.0)
+        ident_b = const.tile([P, P], BF16, name="ident_b")
         cst = const.tile([P, 800], F32, name="cst")
         ancx = [const.tile([P, 32, 2], F32, name="ancx%d" % lvl) for lvl in range(3)]
 
@@ -69,6 +68,8 @@ def tile_head_t_kernel(tc, f0, f1, f2, w0, b0, w1, b1, w2, b2, anchors, out):
         def keep_constants(cps0, cps1):
             nc.vector.tensor_copy(out=cst[:, 0:512], in_=cps0[:])
             nc.vector.tensor_copy(out=cst[:, 512:800], in_=cps1[:, 0:288])
+
+            nc.vector.tensor_copy(out=ident_b[:], in_=ident[:])
 
         def spread_anchors():
             for lvl, rep in ((0, 8), (1, 8), (2, 3)):

@@ -15,18 +15,19 @@ ALU = mybir.AluOpType
 P = 128
 FLOPS = 2 * 256 * (512 * 12 * 1024 + 512 * 12 * 256 + 1024 * 12 * 64)
 
-UNITS = [(0, n) for n in range(6)] + [(1, u) for u in range(3)] + [(0, n) for n in range(6, 9)] + [(2, h) for h in range(2)] + [(0, n) for n in range(9, 12)]
+UNITS = [(0, n) for n in range(0, 6)] + [(1, u) for u in range(3)] + [(0, n) for n in range(6, 12)] + [(2, h) for h in range(3)]
 HEAD_SPLITS = ((44, 44), (60, 60))
-SPLIT = (56, 96)
 PLAIN = (76, 112)
-TENSOR_FROM = 4
-L1_S = 64
-OUT_BUFS = 5
-LOADS = (
-    (-1, "w", 0), (-1, "f0", 0, 1), (-1, "f0", 1, 2), (-1, "f0", 2, 3), (-1, "f0", 3, 4), (-1, "f0", 4, 6), (-1, "w", 1), (-1, "f1",), (-1, "w", 2), (-1, "f0", 6, 9), (3, "f2",), (6, "f0", 9, 12),
-)
-W_PREP = ((1, 3), (2, 8))
+SPLIT = (60, 96)
+TENSOR_FROM = 6
+Q1S = 20
+Q1G = 28
+RAW_BUFS = 8
+OUT_BUFS = 8
+W_STEPS = {1: 3, 2: 9}
+W_AT = {2: 1, 4: 2}
 W_SCALAR = (2,)
+L2_V = ()
 
 
 def tile_head_t_kernel(tc, f0, f1, f2, w0, b0, w1, b1, w2, b2, anchors, out):
@@ -34,9 +35,7 @@ def tile_head_t_kernel(tc, f0, f1, f2, w0, b0, w1, b1, w2, b2, anchors, out):
     with ExitStack() as ctx:
         ctx.enter_context(tc.manual_schedule())
         const = ctx.enter_context(tc.tile_pool(name="const", bufs=1))
-        rawp = ctx.enter_context(tc.tile_pool(name="rawp", bufs=4))
-        midp = ctx.enter_context(tc.tile_pool(name="midp", bufs=1))
-        bigp = ctx.enter_context(tc.tile_pool(name="bigp", bufs=2))
+        rawp = ctx.enter_context(tc.tile_pool(name="rawp", bufs=RAW_BUFS))
         grpp = ctx.enter_context(tc.tile_pool(name="grpp", bufs=2))
         codp = ctx.enter_context(tc.tile_pool(name="codp", bufs=3))
         outp = ctx.enter_context(tc.tile_pool(name="outp", bufs=OUT_BUFS))
@@ -54,6 +53,7 @@ def tile_head_t_kernel(tc, f0, f1, f2, w0, b0, w1, b1, w2, b2, anchors, out):
         ones = const.tile([P, P], BF16, name="ones")
         nc.vector.memset(ones[:], 1.0)
         ident_b = const.tile([P, P], BF16, name="ident_b")
+        perm_b = const.tile([P, P], BF16, name="perm_b")
         cst = const.tile([P, 800], F32, name="cst")
         ancx = [const.tile([P, 32, 2], F32, name="ancx%d" % lvl) for lvl in range(3)]
 
@@ -68,11 +68,14 @@ def tile_head_t_kernel(tc, f0, f1, f2, w0, b0, w1, b1, w2, b2, anchors, out):
         def keep_constants(cps0, cps1):
             nc.vector.tensor_copy(out=cst[:, 0:512], in_=cps0[:])
             nc.vector.tensor_copy(out=cst[:, 512:800], in_=cps1[:, 0:288])
-
             nc.vector.tensor_copy(out=ident_b[:], in_=ident[:])
+            nc.vector.tensor_copy(
+                out=perm_b[:].rearrange("p (m c b r) -> p m c b r", m=4, c=4, b=2, r=4),
+                in_=ident[:].rearrange("p (m b c r) -> p m c b r", m=4, b=2, c=4, r=4),
+            )
 
         def spread_anchors():
-            for lvl, rep in ((0, 8), (1, 8), (2, 3)):
+            for lvl, rep in ((0, 8), (1, 8), (2, 2)):
                 src = cst[:, 768 + 8 * lvl : 776 + 8 * lvl].rearrange("p (a c) -> p a c", a=4).unsqueeze(2)
                 nc.gpsimd.tensor_copy(
                     out=ancx[lvl][:, 0 : 4 * rep, :].rearrange("p (a t) c -> p a t c", a=4),
@@ -85,9 +88,19 @@ def tile_head_t_kernel(tc, f0, f1, f2, w0, b0, w1, b1, w2, b2, anchors, out):
             w, K = ((w0, 512), (w1, 512), (w2, 1024))[lvl]
             w_sb = const.tile([P, 2 * K], BF16, name="w_sb%d" % lvl)
             nc.sync.dma_start(
-                out=w_sb[:].rearrange("o (b k) -> o b k", b=2), in_=w.rearrange("(b o) k -> o b k", b=2)
+                out=w_sb[:], in_=w.rearrange("(o b) k -> o (b k)", b=2)
             )
             wts[lvl] = (w_sb, K)
+
+        def permute_w2():
+            w_sb, K = wts[2]
+            w_pm = const.tile([P, 2 * K], BF16, name="w_pm")
+            src = w_sb[:].bitcast(F32).rearrange("o (b m e c r x) -> o b x m c e r", b=2, m=4, e=2, c=4, r=4, x=4)
+            dst = w_pm[:].bitcast(F32).rearrange("o (b x m c e r) -> o b x m c e r", b=2, x=4, m=4, c=4, e=2, r=4)
+            for b in range(2):
+                for x in range(4):
+                    nc.vector.tensor_copy(out=dst[:, b, x], in_=src[:, b, x])
+            wts["pm"] = w_pm
 
         def turn_w(lvl):
             w_sb, K = wts[lvl]
@@ -95,7 +108,10 @@ def tile_head_t_kernel(tc, f0, f1, f2, w0, b0, w1, b1, w2, b2, anchors, out):
             wc = const.tile([P, passes * 256], U32, name="wc%d" % lvl, align_bytes=64)
             ws = const.tile([P, passes * 256], U8, name="ws%d" % lvl, align_bytes=64)
             wg = const.tile([P, passes * 1024], BF16, name="wg%d" % lvl, align_bytes=64)
-            words = w_sb[:].bitcast(F32).rearrange("o (b g m u) -> o b g u m", b=2, g=passes, m=128, u=2)
+            if lvl == 2:
+                words = wts["pm"][:].bitcast(F32).rearrange("o (b g u m) -> o b g u m", b=2, g=passes, u=2, m=128)
+            else:
+                words = w_sb[:].bitcast(F32).rearrange("o (b g m u) -> o b g u m", b=2, g=passes, m=128, u=2)
             banks = []
             for g in range(passes):
                 xt = psumr.tile([P, 512], F32, tag="rps", name="xt")
@@ -109,48 +125,14 @@ def tile_head_t_kernel(tc, f0, f1, f2, w0, b0, w1, b1, w2, b2, anchors, out):
         def group_w(lvl, on_scalar):
             wc, ws, wg, banks = wts[lvl]
             for g, xt in enumerate(banks):
-                wgv = wg[:, g * 1024 : (g + 1) * 1024].bitcast(F32).rearrange("p (o u) -> p o u", u=2)
-                if on_scalar:
-                    nc.scalar.copy(out=wgv, in_=xt[:].rearrange("p (u o) -> p o u", u=2))
-                else:
-                    nc.vector.tensor_copy(out=wgv, in_=xt[:].rearrange("p (u o) -> p o u", u=2))
+                wgv = wg[:, g * 1024 : (g + 1) * 1024].bitcast(F32).rearrange("p (m b u) -> p m b u", b=2, u=2)
+                copy = nc.scalar.copy if on_scalar else nc.vector.tensor_copy
+                copy(out=wgv, in_=xt[:].rearrange("p (u b m) -> p m b u", u=2, b=2))
 
         def quant_w(lvl):
             wc, ws, wg, banks = wts[lvl]
             nc.vector.quantize_mx(out=wc[:].bitcast(FP8X4), scales=ws[:], in_=wg[:])
             wts[lvl] = (wc, ws)
-
-        raws = {}
-
-        def load_f0(n0, n1):
-            width = 4096 * (n1 - n0)
-            if n1 - n0 == 1:
-                tile = rawp.tile([P, width], BF16, tag="raw", name="raw")
-            elif n1 - n0 == 2:
-                tile = midp.tile([P, width], BF16, tag="mid", name="mid")
-            else:
-                tile = bigp.tile([P, width], BF16, tag="big", name="big")
-            for n in range(n0, n1):
-                raws[n] = (tile, 4096 * (n - n0))
-            nc.sync.dma_start(
-                out=tile[:].rearrange("p (n x) -> p n x", n=n1 - n0),
-                in_=f0[n0:n1].rearrange("n (p j) h w -> p n (j h w)", j=4),
-            )
-
-        def load_f1():
-            raws["f1"] = bigp.tile([P, 12288], BF16, tag="big", name="big")
-            nc.sync.dma_start(
-                out=raws["f1"][:].rearrange("p (n x) -> p n x", n=12),
-                in_=f1.rearrange("n (p j) h w -> p n (j h w)", j=4),
-            )
-
-        def load_f2():
-            raws["f2"] = midp.tile([P, 6144], BF16, tag="mid", name="mid")
-            for g in range(2):
-                nc.sync.dma_start(
-                    out=raws["f2"][:, 3072 * g : 3072 * (g + 1)].rearrange("p (n x) -> p n x", n=12),
-                    in_=f2[:, 512 * g : 512 * (g + 1)].rearrange("n (p j) h w -> p n (j h w)", j=4),
-                )
 
         def pool_copy(dst, src):
             nc.gpsimd.tensor_scalar(out=dst, in0=src, scalar1=1.0, scalar2=0.0, op0=ALU.mult, op1=ALU.add)
@@ -218,8 +200,8 @@ def tile_head_t_kernel(tc, f0, f1, f2, w0, b0, w1, b1, w2, b2, anchors, out):
                     mx(ps[:, 256 * i : 256 * (i + 1)], st, (2 * b + i) * 128, lvl, 0, True, True)
                 st["ps"].append(ps)
 
-        def evac_banks(st, lvl, view):
-            for b in range(4):
+        def evac_banks(st, lvl, banks, view):
+            for b in range(banks):
                 nc.vector.tensor_tensor(
                     out=view(b),
                     in0=st["ps"][b][:].rearrange("p (t a j) -> p a t j", t=2, a=4, j=64),
@@ -235,9 +217,7 @@ def tile_head_t_kernel(tc, f0, f1, f2, w0, b0, w1, b1, w2, b2, anchors, out):
             def turn():
                 if not on_tensor:
                     return
-                tile, c0 = raws[n]
-                raw = tile[:, c0 : c0 + 4096]
-                src_t = raw.rearrange("p (j q t) -> p t q j", j=4, q=128, t=8)
+                src_t = st["raw"][:].rearrange("p (j q t) -> p t q j", j=4, q=128, t=8)
                 st["rps"] = psumr.tile([P, 1024], BF16, tag="rps", name="rps")
                 for th in range(2):
                     nc.tensor.matmul(
@@ -245,33 +225,33 @@ def tile_head_t_kernel(tc, f0, f1, f2, w0, b0, w1, b1, w2, b2, anchors, out):
                         rhs=src_t[:, 4 * th : 4 * th + 4, qg:128, :], start=True, stop=True,
                     )
 
+            def load():
+                st["raw"] = rawp.tile([P, 4096], BF16, tag="raw", name="raw")
+                nc.sync.dma_start(out=st["raw"][:], in_=f0[n].rearrange("(p j) h w -> p (j h w)", j=4))
+
             def regroup():
                 st["grp"] = grpp.tile([P, 4096], BF16, tag="grp", name="grp", align_bytes=64)
-                tile, c0 = raws[n]
-                raw = tile[:, c0 : c0 + 4096]
+                raw = st["raw"][:]
                 src_c = raw.rearrange("p (j q t) -> p q t j", j=4, q=128, t=8)
                 dst_c = st["grp"][:].rearrange("p (t q j) -> p q t j", t=8, q=128, j=4)
-                src_a = raw.rearrange("p (j q t) -> p q j t", j=4, q=128, t=8)
-                dst_a = st["grp"][:].rearrange("p (t q j) -> p q j t", t=8, q=128, j=4)
+                src_a = raw.rearrange("p (j q h t) -> p h q j t", j=4, q=128, h=2, t=4)
+                dst_a = st["grp"][:].rearrange("p (h t q j) -> p h q j t", h=2, t=4, q=128, j=4)
                 halves = (slice(0, 4), slice(4, 8))
                 if on_tensor:
                     nc.scalar.copy(
                         out=st["grp"][:].rearrange("p (t x) -> p t x", t=8)[:, :, 4 * qg : 512],
                         in_=st["rps"][:].rearrange("p (t x) -> p t x", t=8),
                     )
-                for ts in halves:
-                    nc.scalar.copy(out=dst_a[:, 0:qs, :, ts], in_=src_a[:, 0:qs, :, ts])
+                nc.scalar.copy(out=dst_a[:, :, 0:qs], in_=src_a[:, :, 0:qs])
                 for ts in halves if qg > qs else ():
                     pool_copy(dst_c[:, qs:qg, ts, :], src_c[:, qs:qg, ts, :])
-                if on_tensor:
-                    return
-                for ts in halves:
-                    nc.vector.tensor_copy(out=dst_a[:, qg:128, :, ts], in_=src_a[:, qg:128, :, ts])
+                if not on_tensor:
+                    nc.vector.tensor_copy(out=dst_a[:, :, qg:128], in_=src_a[:, :, qg:128])
 
             def evac():
                 st["osb"] = outp.tile([P, 2048], F32, tag="osb", name="osb")
                 ov = st["osb"][:].rearrange("p (a t j) -> p a t j", a=4, t=8, j=64)
-                evac_banks(st, 0, lambda b: ov[:, :, 2 * b : 2 * b + 2, :])
+                evac_banks(st, 0, 4, lambda b: ov[:, :, 2 * b : 2 * b + 2, :])
                 st["rows"] = st["osb"][:].rearrange("p (r j) -> p r j", j=64)
 
             def store():
@@ -281,113 +261,100 @@ def tile_head_t_kernel(tc, f0, f1, f2, w0, b0, w1, b1, w2, b2, anchors, out):
                 )
 
             return {
-                "turn": turn, "regroup": regroup, "mm": lambda: eight_tiles(st, 0), "quant": lambda: quant(st, 4096, ((0, 2048), (2048, 4096))), "evac": evac,
+                "load": load, "turn": turn, "regroup": regroup, "quant": lambda: quant(st, 4096, ((0, 2048), (2048, 4096))),
+                "mm": lambda: eight_tiles(st, 0), "evac": evac,
                 "small_s": lambda: small_s(st), "small_g": lambda: small_g(st, 0), "store": store,
             }
-
-        shared = {}
 
         def make_l1(u):
             st = {}
 
+            def load():
+                st["raw"] = rawp.tile([P, 4096], BF16, tag="raw", name="raw")
+                nc.sync.dma_start(
+                    out=st["raw"][:].rearrange("p (n x) -> p n x", n=4),
+                    in_=f1[4 * u : 4 * u + 4].rearrange("n (p j) h w -> p n (j h w)", j=4),
+                )
+
             def regroup():
                 st["grp"] = grpp.tile([P, 4096], BF16, tag="grp", name="grp", align_bytes=64)
-                for i in range(4):
-                    raw = raws["f1"][:, 1024 * (4 * u + i) : 1024 * (4 * u + i + 1)]
-                    grp = st["grp"][:, 1024 * i : 1024 * (i + 1)]
-                    src = raw.rearrange("p (j v l t) -> p v j l t", j=4, v=64, l=2, t=2)
-                    dst = grp.rearrange("p (t v l j) -> p v j l t", t=2, v=64, l=2, j=4)
-                    if i == 3:
-                        pool_copy(
-                            grp.rearrange("p (t q j) -> p q t j", t=2, q=128, j=4),
-                            raw.rearrange("p (j q t) -> p q t j", j=4, q=128, t=2),
-                        )
-                    elif i == 2:
-                        v = L1_S // 2
-                        nc.scalar.copy(out=dst[:, 0:v], in_=src[:, 0:v])
-                        nc.vector.tensor_copy(out=dst[:, v:64], in_=src[:, v:64])
-                    else:
-                        nc.scalar.copy(out=dst, in_=src)
+                src = st["raw"][:].rearrange("p (i q h t) -> p h q i t", i=16, q=32, h=2, t=4)
+                dst = st["grp"][:].rearrange("p (h t q i) -> p h q i t", h=2, t=4, q=32, i=16)
+                nc.scalar.copy(out=dst[:, :, 0:Q1S], in_=src[:, :, 0:Q1S])
+                for h in range(2):
+                    pool_copy(dst[:, h, Q1S:Q1G], src[:, h, Q1S:Q1G])
+                if Q1G < 32:
+                    nc.vector.tensor_copy(out=dst[:, :, Q1G:32], in_=src[:, :, Q1G:32])
 
             def evac():
-                if u == 0:
-                    shared["o1"] = const.tile([P, 6144], F32, name="o1")
-                ov = shared["o1"][:].rearrange("p (a n t j) -> p a n t j", a=4, n=12, t=2, j=64)
-                evac_banks(st, 1, lambda b: ov[:, :, 4 * u + b, :, :])
-                st["rows"] = shared["o1"][:].rearrange("p (a r j) -> p a r j", a=4, r=24, j=64)[:, :, 8 * u : 8 * u + 8, :]
+                st["osb"] = outp.tile([P, 2048], F32, tag="osb", name="osb")
+                ov = st["osb"][:].rearrange("p (a t j) -> p a t j", a=4, t=8, j=64)
+                evac_banks(st, 1, 4, lambda b: ov[:, :, 2 * b : 2 * b + 2, :])
+                st["rows"] = st["osb"][:].rearrange("p (r j) -> p r j", j=64)
 
             def store():
-                if u < 2:
-                    return
-                for a in range(4):
+                for n in range(4):
                     nc.sync.dma_start(
-                        out=out[:, 4096 + 256 * a : 4096 + 256 * (a + 1), :].rearrange("n (q t) j -> q n (t j)", q=128, t=2),
-                        in_=shared["o1"][:, 1536 * a : 1536 * (a + 1)].rearrange("p (n x) -> p n x", n=12),
+                        out=out[4 * u + n, 4096:5120, :].rearrange("(a q t) j -> q a (t j)", a=4, q=32, t=8),
+                        in_=st["osb"][n:128:4, :].rearrange("p (a x) -> p a x", a=4),
                     )
 
             return {
-                "turn": lambda: None, "regroup": regroup, "mm": lambda: eight_tiles(st, 1), "quant": lambda: quant(st, 4096, ((0, 2048), (2048, 4096))), "evac": evac,
+                "load": load, "turn": lambda: None, "regroup": regroup, "quant": lambda: quant(st, 4096, ((0, 2048), (2048, 4096))),
+                "mm": lambda: eight_tiles(st, 1), "evac": evac,
                 "small_s": lambda: small_s(st), "small_g": lambda: small_g(st, 1), "store": store,
             }
 
         def make_l2(h):
             st = {}
 
+            def load():
+                st["raw"] = rawp.tile([P, 2048], BF16, tag="raw", name="raw")
+                nc.sync.dma_start(
+                    out=st["raw"][:].rearrange("p (n x) -> p n x", n=4),
+                    in_=f2[4 * h : 4 * h + 4].rearrange("n (p j) h w -> p n (j h w)", j=8),
+                )
+
+            def turn():
+                src = st["raw"][:].rearrange("p (n g j q t) -> p g t q n j", n=4, g=2, j=4, q=32, t=2)
+                st["rps"] = []
+                for g in range(2):
+                    rps = psumr.tile([P, 1024], BF16, tag="rps", name="rps")
+                    for t in range(2):
+                        nc.tensor.matmul(
+                            out=rps[:, 512 * t : 512 * (t + 1)], lhsT=perm_b[:], rhs=src[:, g, t], start=True, stop=True
+                        )
+                    st["rps"].append(rps)
+
             def regroup():
-                st["grp"] = grpp.tile([P, 3072], BF16, tag="grp", name="grp", align_bytes=64)
-                src = raws["f2"][:].rearrange("p (g m i v r) -> p g m v i r", g=2, m=6, i=8, v=16, r=4)[:, :, 3 * h : 3 * h + 3]
-                dst = st["grp"][:].rearrange("p (g m v r i) -> p g m v i r", g=2, m=3, v=16, r=4, i=8)
+                st["grp"] = grpp.tile([P, 2048], BF16, tag="grp", name="grp", align_bytes=64)
                 for g in range(2):
-                    nc.scalar.copy(out=dst[:, g, 0], in_=src[:, g, 0])
-                    nc.scalar.copy(out=dst[:, g, 1, 0:8], in_=src[:, g, 1, 0:8])
-                for g in range(2):
-                    pool_copy(dst[:, g, 2], src[:, g, 2])
-                for g in range(2):
-                    nc.vector.tensor_copy(out=dst[:, g, 1, 8:16], in_=src[:, g, 1, 8:16])
+                    copy = nc.vector.tensor_copy if (h, g) in L2_V else nc.scalar.copy
+                    copy(out=st["grp"][:, 1024 * g : 1024 * (g + 1)], in_=st["rps"][g][:])
 
             def mm():
-                st["ps"] = []
-                for b in range(2):
-                    ps = psum.tile([P, 512], F32, tag="bank", name="acc")
-                    for i in range(2 - b):
-                        m = 2 * b + i
-                        for g in range(2):
-                            mx(ps[:, 256 * i : 256 * (i + 1)], st, g * 384 + m * 128, 2, g, g == 0, g == 1)
-                    st["ps"].append(ps)
+                ps = psum.tile([P, 512], F32, tag="bank", name="acc")
+                for t in range(2):
+                    for g in range(2):
+                        mx(ps[:, 256 * t : 256 * (t + 1)], st, g * 256 + t * 128, 2, g, g == 0, g == 1)
+                st["ps"] = [ps]
 
             def evac():
-                if h == 0:
-                    shared["o2"] = const.tile([P, 1536], F32, name="o2")
-                ov = shared["o2"][:].rearrange("p (a m j) -> p a m j", a=4, m=6, j=64)
-                bias = cst[:, 512:768].rearrange("p (a j) -> p a j", a=4)
-                nc.vector.tensor_tensor(
-                    out=ov[:, :, 3 * h : 3 * h + 2, :],
-                    in0=st["ps"][0][:].rearrange("p (m a j) -> p a m j", m=2, a=4),
-                    in1=bias.unsqueeze(2).to_broadcast([P, 4, 2, 64]),
-                    op=ALU.add,
-                )
-                nc.vector.tensor_tensor(
-                    out=ov[:, :, 3 * h + 2, :],
-                    in0=st["ps"][1][:, 0:256].rearrange("p (a j) -> p a j", a=4),
-                    in1=bias,
-                    op=ALU.add,
-                )
-                st["rows"] = ov[:, :, 3 * h : 3 * h + 3, :]
+                st["osb"] = outp.tile([P, 512], F32, tag="osb", name="osb")
+                ov = st["osb"][:].rearrange("p (a t j) -> p a t j", a=4, t=2, j=64)
+                evac_banks(st, 2, 1, lambda b: ov)
+                st["rows"] = st["osb"][:].rearrange("p (r j) -> p r j", j=64)
 
             def store():
-                if h < 1:
-                    return
-                o = out[:, 5120:5376, :].rearrange("(m b) (a s) j -> b a s m j", b=2, a=4)
-                for b in range(2):
-                    for a in range(4):
-                        nc.sync.dma_start(
-                            out=o[b, a],
-                            in_=shared["o2"][b:128:2, 384 * a : 384 * (a + 1)].rearrange("p (m j) -> p m j", m=6),
-                        )
+                for n in range(4):
+                    nc.sync.dma_start(
+                        out=out[4 * h + n, 5120:5376, :].rearrange("(a q t) j -> q a (t j)", a=4, q=32, t=2),
+                        in_=st["osb"][n:128:4, :].rearrange("p (a x) -> p a x", a=4),
+                    )
 
             return {
-                "turn": lambda: None, "regroup": regroup, "mm": mm, "quant": lambda: quant(st, 3072, ((0, 2048), (2048, 3072))), "evac": evac,
-                "small_s": lambda: small_s(st), "small_g": lambda: small_g(st, 2), "store": store,
+                "load": load, "turn": turn, "regroup": regroup, "quant": lambda: quant(st, 2048, ((0, 2048),)), "mm": mm,
+                "evac": evac, "small_s": lambda: small_s(st), "small_g": lambda: small_g(st, 2), "store": store,
             }
 
         units = []
@@ -398,28 +365,22 @@ def tile_head_t_kernel(tc, f0, f1, f2, w0, b0, w1, b1, w2, b2, anchors, out):
                 units.append(make_l1(i) if lvl == 1 else make_l2(i))
         N = len(units)
 
-        def issue(step):
-            for ld in LOADS:
-                if ld[0] == step:
-                    if ld[1] == "w":
-                        load_w(ld[2])
-                    elif ld[1] == "f0":
-                        load_f0(ld[2], ld[3])
-                    elif ld[1] == "f1":
-                        load_f1()
-                    else:
-                        load_f2()
-
-        issue(-1)
+        load_w(0)
+        for i in range(RAW_BUFS):
+            if i in W_AT:
+                load_w(W_AT[i])
+            units[i]["load"]()
         turn_w(0)
         group_w(0, False)
         quant_w(0)
         units[0]["regroup"]()
+        units[RAW_BUFS]["load"]()
         spread = spread_constants()
         units[0]["quant"]()
-        keep_constants(spread[0], spread[1])
         units[0]["mm"]()
+        keep_constants(spread[0], spread[1])
         units[1]["regroup"]()
+        units[RAW_BUFS + 1]["load"]()
         spread_anchors()
         units[2]["turn"]()
 
@@ -436,14 +397,17 @@ def tile_head_t_kernel(tc, f0, f1, f2, w0, b0, w1, b1, w2, b2, anchors, out):
                 units[k + 3]["turn"]()
             if k + 2 < N:
                 units[k + 2]["regroup"]()
+            if k + 2 + RAW_BUFS < N:
+                units[k + 2 + RAW_BUFS]["load"]()
             if 0 <= k - 2 < N:
                 units[k - 2]["small_g"]()
                 units[k - 2]["store"]()
-            issue(k)
-            for lvl, first in W_PREP:
-                if k == first:
+            for lvl in W_STEPS:
+                if lvl == 2 and k == W_STEPS[lvl] - 1:
+                    permute_w2()
+                if k == W_STEPS[lvl]:
                     turn_w(lvl)
-                elif k == first + 1:
+                elif k == W_STEPS[lvl] + 1:
                     group_w(lvl, lvl in W_SCALAR)
-                elif k == first + 2:
+                elif k == W_STEPS[lvl] + 2:
                     quant_w(lvl)

@@ -15,16 +15,14 @@ ALU = mybir.AluOpType
 P = 128
 FLOPS = 2 * 256 * (512 * 12 * 1024 + 512 * 12 * 256 + 1024 * 12 * 64)
 
-UNITS = [(0, n) for n in range(0, 6)] + [(1, u) for u in range(3)] + [(0, n) for n in range(6, 12)] + [(2, h) for h in range(3)]
+UNITS = [(0, 0), (0, 1), (0, 2), (0, 3), (0, 4), (0, 5), (1, 0), (1, 1), (1, 2), (0, 6), (0, 7), (0, 8), (2, 0), (0, 9), (0, 10), (2, 1), (0, 11), (2, 2)]
 HEAD_SPLITS = ((44, 44), (60, 60))
-PLAIN = (76, 112)
-SPLIT = (60, 96)
-TENSOR_FROM = 6
+SPLIT = (76, 116)
 Q1S = 20
 Q1G = 28
 RAW_BUFS = 8
-OUT_BUFS = 8
-W_STEPS = {1: 3, 2: 9}
+OUT_BUFS = 10
+W_STEPS = {1: 3, 2: 6}
 W_AT = {2: 1, 4: 2}
 W_SCALAR = (2,)
 L2_V = ()
@@ -52,7 +50,6 @@ def tile_head_t_kernel(tc, f0, f1, f2, w0, b0, w1, b1, w2, b2, anchors, out):
         make_identity(nc, ident[:])
         ones = const.tile([P, P], BF16, name="ones")
         nc.vector.memset(ones[:], 1.0)
-        ident_b = const.tile([P, P], BF16, name="ident_b")
         perm_b = const.tile([P, P], BF16, name="perm_b")
         cst = const.tile([P, 800], F32, name="cst")
         ancx = [const.tile([P, 32, 2], F32, name="ancx%d" % lvl) for lvl in range(3)]
@@ -68,7 +65,6 @@ def tile_head_t_kernel(tc, f0, f1, f2, w0, b0, w1, b1, w2, b2, anchors, out):
         def keep_constants(cps0, cps1):
             nc.vector.tensor_copy(out=cst[:, 0:512], in_=cps0[:])
             nc.vector.tensor_copy(out=cst[:, 512:800], in_=cps1[:, 0:288])
-            nc.vector.tensor_copy(out=ident_b[:], in_=ident[:])
             nc.vector.tensor_copy(
                 out=perm_b[:].rearrange("p (m c b r) -> p m c b r", m=4, c=4, b=2, r=4),
                 in_=ident[:].rearrange("p (m b c r) -> p m c b r", m=4, b=2, c=4, r=4),
@@ -212,19 +208,6 @@ def tile_head_t_kernel(tc, f0, f1, f2, w0, b0, w1, b1, w2, b2, anchors, out):
         def make_l0(n, split):
             st = {}
             qs, qg = split
-            on_tensor = n >= TENSOR_FROM
-
-            def turn():
-                if not on_tensor:
-                    return
-                src_t = st["raw"][:].rearrange("p (j q t) -> p t q j", j=4, q=128, t=8)
-                st["rps"] = psumr.tile([P, 1024], BF16, tag="rps", name="rps")
-                for th in range(2):
-                    nc.tensor.matmul(
-                        out=st["rps"][:, 512 * th : 512 * (th + 1)], lhsT=ident_b[:],
-                        rhs=src_t[:, 4 * th : 4 * th + 4, qg:128, :], start=True, stop=True,
-                    )
-
             def load():
                 st["raw"] = rawp.tile([P, 4096], BF16, tag="raw", name="raw")
                 nc.sync.dma_start(out=st["raw"][:], in_=f0[n].rearrange("(p j) h w -> p (j h w)", j=4))
@@ -237,16 +220,10 @@ def tile_head_t_kernel(tc, f0, f1, f2, w0, b0, w1, b1, w2, b2, anchors, out):
                 src_a = raw.rearrange("p (j q h t) -> p h q j t", j=4, q=128, h=2, t=4)
                 dst_a = st["grp"][:].rearrange("p (h t q j) -> p h q j t", h=2, t=4, q=128, j=4)
                 halves = (slice(0, 4), slice(4, 8))
-                if on_tensor:
-                    nc.scalar.copy(
-                        out=st["grp"][:].rearrange("p (t x) -> p t x", t=8)[:, :, 4 * qg : 512],
-                        in_=st["rps"][:].rearrange("p (t x) -> p t x", t=8),
-                    )
                 nc.scalar.copy(out=dst_a[:, :, 0:qs], in_=src_a[:, :, 0:qs])
                 for ts in halves if qg > qs else ():
                     pool_copy(dst_c[:, qs:qg, ts, :], src_c[:, qs:qg, ts, :])
-                if not on_tensor:
-                    nc.vector.tensor_copy(out=dst_a[:, :, qg:128], in_=src_a[:, :, qg:128])
+                nc.vector.tensor_copy(out=dst_a[:, :, qg:128], in_=src_a[:, :, qg:128])
 
             def evac():
                 st["osb"] = outp.tile([P, 2048], F32, tag="osb", name="osb")
@@ -261,7 +238,7 @@ def tile_head_t_kernel(tc, f0, f1, f2, w0, b0, w1, b1, w2, b2, anchors, out):
                 )
 
             return {
-                "load": load, "turn": turn, "regroup": regroup, "quant": lambda: quant(st, 4096, ((0, 2048), (2048, 4096))),
+                "load": load, "turn": lambda: None, "regroup": regroup, "quant": lambda: quant(st, 4096, ((0, 2048), (2048, 4096))),
                 "mm": lambda: eight_tiles(st, 0), "evac": evac,
                 "small_s": lambda: small_s(st), "small_g": lambda: small_g(st, 0), "store": store,
             }
@@ -316,13 +293,14 @@ def tile_head_t_kernel(tc, f0, f1, f2, w0, b0, w1, b1, w2, b2, anchors, out):
                 )
 
             def turn():
-                src = st["raw"][:].rearrange("p (n g j q t) -> p g t q n j", n=4, g=2, j=4, q=32, t=2)
+                src = st["raw"][:].rearrange("p (n g x) -> p g n x", n=4, g=2, x=256)
                 st["rps"] = []
                 for g in range(2):
                     rps = psumr.tile([P, 1024], BF16, tag="rps", name="rps")
-                    for t in range(2):
+                    for i in range(2):
                         nc.tensor.matmul(
-                            out=rps[:, 512 * t : 512 * (t + 1)], lhsT=perm_b[:], rhs=src[:, g, t], start=True, stop=True
+                            out=rps[:, 512 * i : 512 * (i + 1)], lhsT=perm_b[:], rhs=src[:, g, 2 * i : 2 * i + 2, :],
+                            start=True, stop=True,
                         )
                     st["rps"].append(rps)
 
@@ -330,7 +308,10 @@ def tile_head_t_kernel(tc, f0, f1, f2, w0, b0, w1, b1, w2, b2, anchors, out):
                 st["grp"] = grpp.tile([P, 2048], BF16, tag="grp", name="grp", align_bytes=64)
                 for g in range(2):
                     copy = nc.vector.tensor_copy if (h, g) in L2_V else nc.scalar.copy
-                    copy(out=st["grp"][:, 1024 * g : 1024 * (g + 1)], in_=st["rps"][g][:])
+                    copy(
+                        out=st["grp"][:, 1024 * g : 1024 * (g + 1)].rearrange("p (t v l i) -> p v i l t", t=2, v=16, l=2, i=16),
+                        in_=st["rps"][g][:].rearrange("p (i v l t) -> p v i l t", i=16, v=16, l=2, t=2),
+                    )
 
             def mm():
                 ps = psum.tile([P, 512], F32, tag="bank", name="acc")
@@ -360,7 +341,7 @@ def tile_head_t_kernel(tc, f0, f1, f2, w0, b0, w1, b1, w2, b2, anchors, out):
         units = []
         for lvl, i in UNITS:
             if lvl == 0:
-                units.append(make_l0(i, HEAD_SPLITS[i] if i < len(HEAD_SPLITS) else PLAIN if i < TENSOR_FROM else SPLIT))
+                units.append(make_l0(i, HEAD_SPLITS[i] if i < len(HEAD_SPLITS) else SPLIT))
             else:
                 units.append(make_l1(i) if lvl == 1 else make_l2(i))
         N = len(units)

@@ -17,14 +17,14 @@ FLOPS = 2 * 256 * (512 * 12 * 1024 + 512 * 12 * 256 + 1024 * 12 * 64)
 
 UNITS = [(0, 0), (0, 1), (0, 2), (0, 3), (0, 4), (0, 5), (1, 0), (1, 1), (1, 2), (0, 6), (0, 7), (0, 8), (2, 0), (0, 9), (0, 10), (2, 1), (0, 11), (2, 2)]
 HEAD_SPLITS = ((44, 44), (60, 60))
-SPLIT = (76, 116)
+SPLIT = (80, 116)
 Q1S = 20
 Q1G = 28
 RAW_BUFS = 8
 OUT_BUFS = 10
 W_STEPS = {1: 3, 2: 6}
 W_AT = {2: 1, 4: 2}
-W_SCALAR = (2,)
+W_SCALAR = (1, 2)
 L2_V = ()
 
 

from contextlib import ExitStack

import concourse.mybir as mybir
from concourse.masks import make_identity

F32 = mybir.dt.float32
BF16 = mybir.dt.bfloat16
I32 = mybir.dt.int32
U32 = mybir.dt.uint32
U8 = mybir.dt.uint8
FP8X4 = mybir.dt.float8_e4m3fn_x4
ACT = mybir.ActivationFunctionType
ALU = mybir.AluOpType

P = 128
FLOPS = 2 * 256 * (512 * 12 * 1024 + 512 * 12 * 256 + 1024 * 12 * 64)

UNITS = [(0, 0), (0, 1), (0, 2), (0, 3), (0, 4), (0, 5), (1, 0), (1, 1), (1, 2), (0, 6), (0, 7), (0, 8), (2, 0), (0, 9), (0, 10), (2, 1), (0, 11), (2, 2)]
HEAD_SPLITS = ((44, 44), (60, 60))
SPLIT = (80, 116)
Q1S = 20
Q1G = 28
RAW_BUFS = 8
OUT_BUFS = 10
W_STEPS = {1: 3, 2: 6}
W_AT = {2: 1, 4: 2}
W_SCALAR = (1, 2)
L2_V = ()


def tile_head_t_kernel(tc, f0, f1, f2, w0, b0, w1, b1, w2, b2, anchors, out):
    nc = tc.nc
    with ExitStack() as ctx:
        ctx.enter_context(tc.manual_schedule())
        const = ctx.enter_context(tc.tile_pool(name="const", bufs=1))
        rawp = ctx.enter_context(tc.tile_pool(name="rawp", bufs=RAW_BUFS))
        grpp = ctx.enter_context(tc.tile_pool(name="grpp", bufs=2))
        codp = ctx.enter_context(tc.tile_pool(name="codp", bufs=3))
        outp = ctx.enter_context(tc.tile_pool(name="outp", bufs=OUT_BUFS))
        smallp = ctx.enter_context(tc.tile_pool(name="smallp", bufs=3))
        psum = ctx.enter_context(tc.psum_pool(name="psum", bufs=6))
        psumr = ctx.enter_context(tc.psum_pool(name="psumr", bufs=2))

        crow = const.tile([P, 800], BF16, name="crow")
        nc.vector.memset(crow[:].bitcast(I32), 0)
        for i, b in enumerate((b0, b1, b2)):
            nc.scalar.dma_start(out=crow[0:1, 256 * i : 256 * (i + 1)], in_=b.unsqueeze(0))
        nc.scalar.dma_start(out=crow[0:1, 768:792], in_=anchors.rearrange("l a c -> (l a c)").unsqueeze(0))
        ident = const.tile([P, P], F32, name="ident")
        make_identity(nc, ident[:])
        ones = const.tile([P, P], BF16, name="ones")
        nc.vector.memset(ones[:], 1.0)
        perm_b = const.tile([P, P], BF16, name="perm_b")
        cst = const.tile([P, 800], F32, name="cst")
        ancx = [const.tile([P, 32, 2], F32, name="ancx%d" % lvl) for lvl in range(3)]

        def spread_constants():
            cps0 = psum.tile([P, 512], F32, tag="bank", name="cps0")
            nc.tensor.matmul(out=cps0[:], lhsT=ones[:], rhs=crow[:, 0:512], start=True, stop=True)
            cps1 = psum.tile([P, 512], F32, tag="bank", name="cps1")
            nc.tensor.matmul(out=cps1[:, 0:256], lhsT=ones[:], rhs=crow[:, 512:768], start=True, stop=True)
            nc.tensor.matmul(out=cps1[:, 256:288], lhsT=ones[:], rhs=crow[:, 768:800], start=True, stop=True)
            return cps0, cps1

        def keep_constants(cps0, cps1):
            nc.vector.tensor_copy(out=cst[:, 0:512], in_=cps0[:])
            nc.vector.tensor_copy(out=cst[:, 512:800], in_=cps1[:, 0:288])
            nc.vector.tensor_copy(
                out=perm_b[:].rearrange("p (m c b r) -> p m c b r", m=4, c=4, b=2, r=4),
                in_=ident[:].rearrange("p (m b c r) -> p m c b r", m=4, b=2, c=4, r=4),
            )

        def spread_anchors():
            for lvl, rep in ((0, 8), (1, 8), (2, 2)):
                src = cst[:, 768 + 8 * lvl : 776 + 8 * lvl].rearrange("p (a c) -> p a c", a=4).unsqueeze(2)
                nc.gpsimd.tensor_copy(
                    out=ancx[lvl][:, 0 : 4 * rep, :].rearrange("p (a t) c -> p a t c", a=4),
                    in_=src.to_broadcast([P, 4, rep, 2]),
                )

        wts = {}

        def load_w(lvl):
            w, K = ((w0, 512), (w1, 512), (w2, 1024))[lvl]
            w_sb = const.tile([P, 2 * K], BF16, name="w_sb%d" % lvl)
            nc.sync.dma_start(
                out=w_sb[:], in_=w.rearrange("(o b) k -> o (b k)", b=2)
            )
            wts[lvl] = (w_sb, K)

        def permute_w2():
            w_sb, K = wts[2]
            w_pm = const.tile([P, 2 * K], BF16, name="w_pm")
            src = w_sb[:].bitcast(F32).rearrange("o (b m e c r x) -> o b x m c e r", b=2, m=4, e=2, c=4, r=4, x=4)
            dst = w_pm[:].bitcast(F32).rearrange("o (b x m c e r) -> o b x m c e r", b=2, x=4, m=4, c=4, e=2, r=4)
            for b in range(2):
                for x in range(4):
                    nc.vector.tensor_copy(out=dst[:, b, x], in_=src[:, b, x])
            wts["pm"] = w_pm

        def turn_w(lvl):
            w_sb, K = wts[lvl]
            passes = K // 512
            wc = const.tile([P, passes * 256], U32, name="wc%d" % lvl, align_bytes=64)
            ws = const.tile([P, passes * 256], U8, name="ws%d" % lvl, align_bytes=64)
            wg = const.tile([P, passes * 1024], BF16, name="wg%d" % lvl, align_bytes=64)
            if lvl == 2:
                words = wts["pm"][:].bitcast(F32).rearrange("o (b g u m) -> o b g u m", b=2, g=passes, u=2, m=128)
            else:
                words = w_sb[:].bitcast(F32).rearrange("o (b g m u) -> o b g u m", b=2, g=passes, m=128, u=2)
            banks = []
            for g in range(passes):
                xt = psumr.tile([P, 512], F32, tag="rps", name="xt")
                banks.append(xt)
                for u in range(2):
                    for b in range(2):
                        c0 = u * 256 + b * 128
                        nc.tensor.transpose(xt[:, c0 : c0 + 128], words[:, b, g, u, :], ident[:])
            wts[lvl] = (wc, ws, wg, banks)

        def group_w(lvl, on_scalar):
            wc, ws, wg, banks = wts[lvl]
            for g, xt in enumerate(banks):
                wgv = wg[:, g * 1024 : (g + 1) * 1024].bitcast(F32).rearrange("p (m b u) -> p m b u", b=2, u=2)
                copy = nc.scalar.copy if on_scalar else nc.vector.tensor_copy
                copy(out=wgv, in_=xt[:].rearrange("p (u b m) -> p m b u", u=2, b=2))

        def quant_w(lvl):
            wc, ws, wg, banks = wts[lvl]
            nc.vector.quantize_mx(out=wc[:].bitcast(FP8X4), scales=ws[:], in_=wg[:])
            wts[lvl] = (wc, ws)

        def pool_copy(dst, src):
            nc.gpsimd.tensor_scalar(out=dst, in0=src, scalar1=1.0, scalar2=0.0, op0=ALU.mult, op1=ALU.add)

        def mx(ps_cols, st, c0, lvl, g, start, stop):
            wc, ws = wts[lvl]
            nc.tensor.matmul_mx(
                out=ps_cols,
                lhsT=st["cod"][:, c0 : c0 + 128].bitcast(FP8X4),
                lhsT_scale=st["scl"][:, c0 : c0 + 128],
                rhs=wc[:, g * 256 : (g + 1) * 256].bitcast(FP8X4),
                rhs_scale=ws[:, g * 256 : (g + 1) * 256],
                start=start,
                stop=stop,
            )

        def fields(ap, lo, hi):
            return ap[:, :, lo:hi] if len(ap.shape) == 3 else ap[:, :, :, lo:hi]

        def small_s(st):
            rows = st["rows"]
            d = list(rows.shape[1:-1])
            n = d[0] * (d[1] if len(d) > 1 else 1)
            sg = smallp.tile([P, 32, 4], F32, tag="sg", name="sg")
            sq = smallp.tile([P, 32, 2], F32, tag="sq", name="sq")
            sgv, sqv = sg[:, 0:n, :], sq[:, 0:n, :]
            if len(d) > 1:
                sgv = sgv.rearrange("p (a r) c -> p a r c", a=d[0])
                sqv = sqv.rearrange("p (a r) c -> p a r c", a=d[0])
            nc.scalar.activation(out=sgv, in_=fields(rows, 0, 4), func=ACT.Sigmoid)
            nc.scalar.activation(out=fields(rows, 0, 2), in_=fields(sgv, 0, 2), func=ACT.Copy, scale=2.0, bias=-0.5)
            nc.scalar.activation(out=sqv, in_=fields(sgv, 2, 4), func=ACT.Square, scale=2.0)
            st["sq"] = (sqv, n, d)

        def small_g(st, lvl):
            sqv, n, d = st["sq"]
            anc = ancx[lvl][:, 0:n, :]
            if len(d) > 1:
                anc = anc.rearrange("p (a r) c -> p a r c", a=d[0])
            nc.gpsimd.tensor_tensor(out=fields(st["rows"], 2, 4), in0=sqv, in1=anc, op=ALU.mult)

        def bias_at(lvl):
            return (
                cst[:, 256 * lvl : 256 * (lvl + 1)]
                .rearrange("p (a j) -> p a j", a=4)
                .unsqueeze(2)
                .to_broadcast([P, 4, 2, 64])
            )

        def quant(st, width, cuts):
            st["cod"] = codp.tile([P, width // 4], U32, tag="cod", name="cod", align_bytes=64)
            st["scl"] = codp.tile([P, width // 4], U8, tag="scl", name="scl", align_bytes=64)
            for lo, hi in cuts:
                nc.vector.quantize_mx(
                    out=st["cod"][:, lo // 4 : hi // 4].bitcast(FP8X4),
                    scales=st["scl"][:, lo // 4 : hi // 4],
                    in_=st["grp"][:, lo:hi],
                )

        def eight_tiles(st, lvl):
            st["ps"] = []
            for b in range(4):
                ps = psum.tile([P, 512], F32, tag="bank", name="acc")
                for i in range(2):
                    mx(ps[:, 256 * i : 256 * (i + 1)], st, (2 * b + i) * 128, lvl, 0, True, True)
                st["ps"].append(ps)

        def evac_banks(st, lvl, banks, view):
            for b in range(banks):
                nc.vector.tensor_tensor(
                    out=view(b),
                    in0=st["ps"][b][:].rearrange("p (t a j) -> p a t j", t=2, a=4, j=64),
                    in1=bias_at(lvl),
                    op=ALU.add,
                )

        def make_l0(n, split):
            st = {}
            qs, qg = split
            def load():
                st["raw"] = rawp.tile([P, 4096], BF16, tag="raw", name="raw")
                nc.sync.dma_start(out=st["raw"][:], in_=f0[n].rearrange("(p j) h w -> p (j h w)", j=4))

            def regroup():
                st["grp"] = grpp.tile([P, 4096], BF16, tag="grp", name="grp", align_bytes=64)
                raw = st["raw"][:]
                src_c = raw.rearrange("p (j q t) -> p q t j", j=4, q=128, t=8)
                dst_c = st["grp"][:].rearrange("p (t q j) -> p q t j", t=8, q=128, j=4)
                src_a = raw.rearrange("p (j q h t) -> p h q j t", j=4, q=128, h=2, t=4)
                dst_a = st["grp"][:].rearrange("p (h t q j) -> p h q j t", h=2, t=4, q=128, j=4)
                halves = (slice(0, 4), slice(4, 8))
                nc.scalar.copy(out=dst_a[:, :, 0:qs], in_=src_a[:, :, 0:qs])
                for ts in halves if qg > qs else ():
                    pool_copy(dst_c[:, qs:qg, ts, :], src_c[:, qs:qg, ts, :])
                nc.vector.tensor_copy(out=dst_a[:, :, qg:128], in_=src_a[:, :, qg:128])

            def evac():
                st["osb"] = outp.tile([P, 2048], F32, tag="osb", name="osb")
                ov = st["osb"][:].rearrange("p (a t j) -> p a t j", a=4, t=8, j=64)
                evac_banks(st, 0, 4, lambda b: ov[:, :, 2 * b : 2 * b + 2, :])
                st["rows"] = st["osb"][:].rearrange("p (r j) -> p r j", j=64)

            def store():
                nc.sync.dma_start(
                    out=out[n, 0:4096, :].rearrange("(a q t) j -> q a (t j)", a=4, q=128, t=8),
                    in_=st["osb"][:].rearrange("p (a x) -> p a x", a=4),
                )

            return {
                "load": load, "turn": lambda: None, "regroup": regroup, "quant": lambda: quant(st, 4096, ((0, 2048), (2048, 4096))),
                "mm": lambda: eight_tiles(st, 0), "evac": evac,
                "small_s": lambda: small_s(st), "small_g": lambda: small_g(st, 0), "store": store,
            }

        def make_l1(u):
            st = {}

            def load():
                st["raw"] = rawp.tile([P, 4096], BF16, tag="raw", name="raw")
                nc.sync.dma_start(
                    out=st["raw"][:].rearrange("p (n x) -> p n x", n=4),
                    in_=f1[4 * u : 4 * u + 4].rearrange("n (p j) h w -> p n (j h w)", j=4),
                )

            def regroup():
                st["grp"] = grpp.tile([P, 4096], BF16, tag="grp", name="grp", align_bytes=64)
                src = st["raw"][:].rearrange("p (i q h t) -> p h q i t", i=16, q=32, h=2, t=4)
                dst = st["grp"][:].rearrange("p (h t q i) -> p h q i t", h=2, t=4, q=32, i=16)
                nc.scalar.copy(out=dst[:, :, 0:Q1S], in_=src[:, :, 0:Q1S])
                for h in range(2):
                    pool_copy(dst[:, h, Q1S:Q1G], src[:, h, Q1S:Q1G])
                if Q1G < 32:
                    nc.vector.tensor_copy(out=dst[:, :, Q1G:32], in_=src[:, :, Q1G:32])

            def evac():
                st["osb"] = outp.tile([P, 2048], F32, tag="osb", name="osb")
                ov = st["osb"][:].rearrange("p (a t j) -> p a t j", a=4, t=8, j=64)
                evac_banks(st, 1, 4, lambda b: ov[:, :, 2 * b : 2 * b + 2, :])
                st["rows"] = st["osb"][:].rearrange("p (r j) -> p r j", j=64)

            def store():
                for n in range(4):
                    nc.sync.dma_start(
                        out=out[4 * u + n, 4096:5120, :].rearrange("(a q t) j -> q a (t j)", a=4, q=32, t=8),
                        in_=st["osb"][n:128:4, :].rearrange("p (a x) -> p a x", a=4),
                    )

            return {
                "load": load, "turn": lambda: None, "regroup": regroup, "quant": lambda: quant(st, 4096, ((0, 2048), (2048, 4096))),
                "mm": lambda: eight_tiles(st, 1), "evac": evac,
                "small_s": lambda: small_s(st), "small_g": lambda: small_g(st, 1), "store": store,
            }

        def make_l2(h):
            st = {}

            def load():
                st["raw"] = rawp.tile([P, 2048], BF16, tag="raw", name="raw")
                nc.sync.dma_start(
                    out=st["raw"][:].rearrange("p (n x) -> p n x", n=4),
                    in_=f2[4 * h : 4 * h + 4].rearrange("n (p j) h w -> p n (j h w)", j=8),
                )

            def turn():
                src = st["raw"][:].rearrange("p (n g x) -> p g n x", n=4, g=2, x=256)
                st["rps"] = []
                for g in range(2):
                    rps = psumr.tile([P, 1024], BF16, tag="rps", name="rps")
                    for i in range(2):
                        nc.tensor.matmul(
                            out=rps[:, 512 * i : 512 * (i + 1)], lhsT=perm_b[:], rhs=src[:, g, 2 * i : 2 * i + 2, :],
                            start=True, stop=True,
                        )
                    st["rps"].append(rps)

            def regroup():
                st["grp"] = grpp.tile([P, 2048], BF16, tag="grp", name="grp", align_bytes=64)
                for g in range(2):
                    copy = nc.vector.tensor_copy if (h, g) in L2_V else nc.scalar.copy
                    copy(
                        out=st["grp"][:, 1024 * g : 1024 * (g + 1)].rearrange("p (t v l i) -> p v i l t", t=2, v=16, l=2, i=16),
                        in_=st["rps"][g][:].rearrange("p (i v l t) -> p v i l t", i=16, v=16, l=2, t=2),
                    )

            def mm():
                ps = psum.tile([P, 512], F32, tag="bank", name="acc")
                for t in range(2):
                    for g in range(2):
                        mx(ps[:, 256 * t : 256 * (t + 1)], st, g * 256 + t * 128, 2, g, g == 0, g == 1)
                st["ps"] = [ps]

            def evac():
                st["osb"] = outp.tile([P, 512], F32, tag="osb", name="osb")
                ov = st["osb"][:].rearrange("p (a t j) -> p a t j", a=4, t=2, j=64)
                evac_banks(st, 2, 1, lambda b: ov)
                st["rows"] = st["osb"][:].rearrange("p (r j) -> p r j", j=64)

            def store():
                for n in range(4):
                    nc.sync.dma_start(
                        out=out[4 * h + n, 5120:5376, :].rearrange("(a q t) j -> q a (t j)", a=4, q=32, t=2),
                        in_=st["osb"][n:128:4, :].rearrange("p (a x) -> p a x", a=4),
                    )

            return {
                "load": load, "turn": turn, "regroup": regroup, "quant": lambda: quant(st, 2048, ((0, 2048),)), "mm": mm,
                "evac": evac, "small_s": lambda: small_s(st), "small_g": lambda: small_g(st, 2), "store": store,
            }

        units = []
        for lvl, i in UNITS:
            if lvl == 0:
                units.append(make_l0(i, HEAD_SPLITS[i] if i < len(HEAD_SPLITS) else SPLIT))
            else:
                units.append(make_l1(i) if lvl == 1 else make_l2(i))
        N = len(units)

        load_w(0)
        for i in range(RAW_BUFS):
            if i in W_AT:
                load_w(W_AT[i])
            units[i]["load"]()
        turn_w(0)
        group_w(0, False)
        quant_w(0)
        units[0]["regroup"]()
        units[RAW_BUFS]["load"]()
        spread = spread_constants()
        units[0]["quant"]()
        units[0]["mm"]()
        keep_constants(spread[0], spread[1])
        units[1]["regroup"]()
        units[RAW_BUFS + 1]["load"]()
        spread_anchors()
        units[2]["turn"]()

        for k in range(N + 2):
            if 0 <= k - 2 < N:
                units[k - 2]["small_s"]()
            if 0 < k < N:
                units[k]["quant"]()
            if 0 <= k - 1 < N:
                units[k - 1]["evac"]()
            if 0 < k < N:
                units[k]["mm"]()
            if k + 3 < N:
                units[k + 3]["turn"]()
            if k + 2 < N:
                units[k + 2]["regroup"]()
            if k + 2 + RAW_BUFS < N:
                units[k + 2 + RAW_BUFS]["load"]()
            if 0 <= k - 2 < N:
                units[k - 2]["small_g"]()
                units[k - 2]["store"]()
            for lvl in W_STEPS:
                if lvl == 2 and k == W_STEPS[lvl] - 1:
                    permute_w2()
                if k == W_STEPS[lvl]:
                    turn_w(lvl)
                elif k == W_STEPS[lvl] + 1:
                    group_w(lvl, lvl in W_SCALAR)
                elif k == W_STEPS[lvl] + 2:
                    quant_w(lvl)
